import numpy as np
import ml_dtypes


def mxq(x, axis, fmt="e4m3"):
    dtype, down = {"e4m3": (ml_dtypes.float8_e4m3fn, 7), "e5m2": (ml_dtypes.float8_e5m2, 14)}[fmt]
    v = np.moveaxis(np.asarray(x, np.float32).astype(ml_dtypes.bfloat16).astype(np.float64), axis, -1)
    blocks = v.reshape(v.shape[:-1] + (-1, 32))
    amax = np.abs(blocks).max(-1, keepdims=True)
    byte = np.maximum(np.where(amax > 0, np.frexp(amax)[1] - 1 + 127, 0) - down, 1)
    scale = np.exp2(byte - 127.0)
    codes = (blocks / scale).astype(np.float32).astype(dtype).astype(np.float64)
    return np.moveaxis((codes * scale).reshape(v.shape), -1, axis)


WIDE = False


def mx_kscale(k):
    if not WIDE:
        return np.ones(k)
    levels = np.array([10, -10, 5, -5, 0])
    a = np.random.permutation(np.resize(levels, k // 512 * 4)).reshape(k // 512, 4)
    idx = np.arange(k)
    return np.exp2(a[idx // 512, idx % 128 // 32])


BF16 = ml_dtypes.bfloat16


def bf(x):
    return np.asarray(x, np.float32).astype(BF16)


def f64(x):
    return np.asarray(x).astype(np.float64)


B, S, H, E, V, G, P = 8, 512, 1024, 512, 256, 5, 3
C = G + P
KNOTS = np.linspace(-1.0 - 2.0 / G * P, 1.0 + 2.0 / G * P, G + 2 * P + 1)


def silu(v):
    e = np.exp(-np.abs(v))
    return v * np.where(v >= 0.0, 1.0, e) / (1.0 + e)


def b_splines(x):
    xe = x[..., None]
    bases = np.where((xe >= KNOTS[:-1]) & (xe < KNOTS[1:]), 1.0, 0.0)
    for p in range(1, P + 1):
        left = (xe - KNOTS[: -(p + 1)]) / (KNOTS[p:-1] - KNOTS[: -(p + 1)])
        right = (KNOTS[p + 1:] - xe) / (KNOTS[p + 1:] - KNOTS[1:-p])
        bases = left * bases[..., :-1] + right * bases[..., 1:]
    return bases


def setup_inputs():
    s = mx_kscale(E)
    u = s / s.min()
    return {"h_norm": bf(np.random.standard_normal((B, S, E)) * u),
            "base_w2": bf(np.random.standard_normal((V, E)) / np.sqrt(E) / u),
            "spline_w2": bf(np.random.standard_normal((V, E, C)) / np.sqrt(E))}


def reference(h_norm, base_w2, spline_w2):
    x = f64(h_norm).reshape(B * S, E)
    base = mxq(silu(x), 1, "e4m3") @ mxq(f64(base_w2), 1, "e4m3").T
    spl = mxq(b_splines(x).reshape(B * S, E * C), 1, "e4m3") @ mxq(f64(spline_w2).reshape(V, E * C), 1, "e4m3").T
    return (base + spl).reshape(B, S, V)

@@ -1,0 +1,188 @@
+import math
+
+import concourse.mybir as mybir
+from concourse.masks import make_identity
+
+F32 = mybir.dt.float32
+BF16 = mybir.dt.bfloat16
+U32 = mybir.dt.uint32
+U8 = mybir.dt.uint8
+FP8X4 = mybir.dt.float8_e4m3fn_x4
+ACT = mybir.ActivationFunctionType
+ALU = mybir.AluOpType
+
+P = 128
+PACK = 4
+TOKENS = 8 * 512
+FEATURES = 512
+OUTPUTS = 256
+BASIS = 8
+PAIRS = BASIS // 2
+PASSES = 1 + BASIS
+TILES = 4
+CHUNK = TILES * P
+COLS = CHUNK * PACK
+HALVES = 2
+
+FLOPS = 2 * TOKENS * OUTPUTS * FEATURES * PASSES
+
+
+def pass_of(c):
+    return 1 + 2 * (c % PAIRS) + c // PAIRS
+
+
+def tile_generatorhead_pb_t_kernel(tc, h_norm, base_w2, spline_w2, out):
+    nc = tc.nc
+    x = h_norm.flatten_outer_dims()
+    y = out.flatten_outer_dims()
+
+    with tc.tile_pool(name="const", bufs=1) as const, tc.tile_pool(
+        name="weights", bufs=1
+    ) as weights, tc.tile_pool(name="stage", bufs=2) as stage, tc.tile_pool(
+        name="work", bufs=2
+    ) as work, tc.psum_pool(name="turned", bufs=3) as turned, tc.psum_pool(
+        name="sums", bufs=3
+    ) as sums:
+        ident = const.tile([P, P], F32)
+        make_identity(nc, ident[:])
+
+        k_outer = 1.0 / math.sqrt(6.0)
+        ones = const.tile([P, 1], F32)
+        nc.vector.memset(ones[:], 1.0)
+        outer_bias = const.tile([P, 1], F32)
+        nc.vector.tensor_scalar(
+            out=outer_bias[:], in0=ones[:], scalar1=-2.0 * k_outer, scalar2=None, op0=ALU.mult
+        )
+
+        def turn_words(rows_of, grouped):
+            bank = turned.tile([P, 2, HALVES, P], F32, tag="bank")
+            for n in range(2):
+                words = rows_of(n).bitcast(F32)
+                for u in range(HALVES):
+                    nc.tensor.transpose(bank[:, n, u, :], words[:, u * P : (u + 1) * P], ident[:])
+            nc.scalar.copy(
+                out=grouped.bitcast(F32).rearrange("p (n r) u -> p n r u", n=2),
+                in_=bank[:].rearrange("p n u r -> p n r u"),
+            )
+
+        base_raw = weights.tile([P, 2, FEATURES], BF16)
+        nc.sync.dma_start(out=base_raw[:], in_=base_w2.rearrange("(n o) i -> o n i", n=2))
+        spline_raw = weights.tile([P, 2, FEATURES * BASIS], BF16)
+        nc.sync.dma_start(
+            out=spline_raw[:], in_=spline_w2.rearrange("(n o) i c -> o n (i c)", n=2)
+        )
+        spline_by_c = weights.tile([P, 2, BASIS, FEATURES], BF16)
+        for n in range(2):
+            nc.vector.tensor_copy(
+                out=spline_by_c[:, n, :, :],
+                in_=spline_raw[:, n, :].rearrange("o (i c) -> o c i", c=BASIS),
+            )
+        w_codes = weights.tile([P, PASSES, OUTPUTS], U32, align_bytes=64)
+        w_scales = weights.tile([P, PASSES, OUTPUTS], U8, align_bytes=64)
+
+        def quantise_weight(q, rows_of):
+            w_grouped = stage.tile([P, OUTPUTS, PACK], BF16, align_bytes=64)
+            turn_words(rows_of, w_grouped[:])
+            nc.vector.quantize_mx(
+                out=w_codes[:, q, :].bitcast(FP8X4),
+                scales=w_scales[:, q, :],
+                in_=w_grouped[:].rearrange("p o t -> p (o t)"),
+            )
+
+        quantise_weight(0, lambda n: base_raw[:, n, :])
+        for c in range(BASIS):
+            quantise_weight(pass_of(c), lambda n, c=c: spline_by_c[:, n, c, :])
+
+        for first in range(0, TOKENS, CHUNK):
+            x_raw = stage.tile([P, TILES, FEATURES], BF16)
+            nc.sync.dma_start(
+                out=x_raw[:], in_=x[first : first + CHUNK, :].rearrange("(p j) i -> p j i", j=TILES)
+            )
+            x_grouped = stage.tile([P, CHUNK, PACK], BF16)
+            for j in range(0, TILES, 2):
+                turn_words(
+                    lambda n, j=j: x_raw[:, j + n, :], x_grouped[:, j * P : (j + 2) * P, :]
+                )
+            xt = x_grouped[:].rearrange("p s t -> p (s t)")
+
+            codes = stage.tile([P, PASSES, CHUNK], U32, align_bytes=64)
+            scales = stage.tile([P, PASSES, CHUNK], U8, align_bytes=64)
+
+            silu = work.tile([P, COLS], BF16, align_bytes=64)
+            nc.scalar.activation(out=silu[:], in_=xt, func=ACT.Silu)
+            nc.vector.quantize_mx(
+                out=codes[:, 0, :].bitcast(FP8X4), scales=scales[:, 0, :], in_=silu[:]
+            )
+
+            for r in range(PAIRS):
+                dist = work.tile([P, COLS], F32)
+                nc.scalar.activation(
+                    out=dist[:], in_=xt, func=ACT.Abs, scale=2.5, bias=1.5 - r
+                )
+                nc.scalar.activation(out=dist[:], in_=dist[:], func=ACT.Abs, bias=-2.0)
+                sq_mid = work.tile([P, COLS], F32)
+                nc.scalar.activation(
+                    out=sq_mid[:], in_=dist[:], func=ACT.Square, scale=1.0 / math.sqrt(2.0)
+                )
+                sq_out = work.tile([P, COLS], F32)
+                nc.scalar.activation(
+                    out=sq_out[:], in_=dist[:], func=ACT.Square, scale=k_outer, bias=outer_bias[:]
+                )
+
+                nc.vector.scalar_tensor_tensor(
+                    out=sq_mid[:], in0=dist[:], scalar=2.0, in1=sq_mid[:],
+                    op0=ALU.subtract, op1=ALU.mult,
+                )
+                neg_mid = work.tile([P, COLS], BF16)
+                nc.vector.tensor_scalar(
+                    out=neg_mid[:], in0=sq_mid[:], scalar1=-1.0, scalar2=-2.0 / 3.0,
+                    op0=ALU.mult, op1=ALU.add,
+                )
+                neg_out = work.tile([P, COLS], BF16)
+                nc.vector.scalar_tensor_tensor(
+                    out=neg_out[:], in0=dist[:], scalar=2.0, in1=sq_out[:],
+                    op0=ALU.subtract, op1=ALU.mult,
+                )
+                nc.vector.tensor_tensor(out=neg_mid[:], in0=neg_mid[:], in1=neg_out[:], op=ALU.max)
+                nc.vector.tensor_scalar_min(out=neg_mid[:], in0=neg_mid[:], scalar1=0.0)
+                side = work.tile([P, COLS], BF16)
+                nc.vector.tensor_scalar(
+                    out=side[:], in0=xt, scalar1=-2.2 + 0.4 * (r + PAIRS), scalar2=0.5,
+                    op0=ALU.is_lt, op1=ALU.subtract,
+                )
+                nc.vector.tensor_tensor(out=side[:], in0=neg_mid[:], in1=side[:], op=ALU.mult)
+                pair = work.tile([P, 2, COLS], BF16, align_bytes=64)
+                nc.vector.tensor_scalar(
+                    out=pair[:, 0, :], in0=side[:], scalar1=-2.0, scalar2=0.0,
+                    op0=ALU.mult, op1=ALU.max,
+                )
+                nc.vector.tensor_scalar(
+                    out=pair[:, 1, :], in0=side[:], scalar1=2.0, scalar2=0.0,
+                    op0=ALU.mult, op1=ALU.max,
+                )
+                q = pass_of(r)
+                nc.vector.quantize_mx(
+                    out=codes[:, q : q + 2, :].rearrange("p q s -> p (q s)").bitcast(FP8X4),
+                    scales=scales[:, q : q + 2, :].rearrange("p q s -> p (q s)"),
+                    in_=pair[:].rearrange("p h f -> p (h f)"),
+                )
+
+            result = stage.tile([P, TILES, OUTPUTS], F32)
+            for j in range(TILES):
+                slots = slice(j * P, (j + 1) * P)
+                acc = sums.tile([P, OUTPUTS], F32)
+                for q in range(PASSES):
+                    nc.tensor.matmul_mx(
+                        out=acc[:],
+                        lhsT=codes[:, q, slots].bitcast(FP8X4),
+                        lhsT_scale=scales[:, q, slots],
+                        rhs=w_codes[:, q, :].bitcast(FP8X4),
+                        rhs_scale=w_scales[:, q, :],
+                        start=(q == 0),
+                        stop=(q == PASSES - 1),
+                    )
+                nc.scalar.copy(out=result[:, j, :], in_=acc[:])
+            nc.sync.dma_start(
+                out=y[first : first + CHUNK, :].rearrange("(p j) o -> p j o", j=TILES),
+                in_=result[:],
+            )

@@ -1,4 +1,5 @@
 import math
+from contextlib import ExitStack
 
 import concourse.mybir as mybir
 from concourse.masks import make_identity
@@ -18,9 +19,11 @@ FEATURES = 512
 OUTPUTS = 256
 BASIS = 8
 PAIRS = BASIS // 2
-PASSES = 1 + BASIS
-TILES = 4
+PASSES = BASIS + 1
+SILU_PASS = BASIS
+TILES = 2
 CHUNK = TILES * P
+CHUNKS = TOKENS // CHUNK
 COLS = CHUNK * PACK
 HALVES = 2
 
@@ -28,7 +31,7 @@ FLOPS = 2 * TOKENS * OUTPUTS * FEATURES * PASSES
 
 
 def pass_of(c):
-    return 1 + 2 * (c % PAIRS) + c // PAIRS
+    return 2 * (c % PAIRS) + c // PAIRS
 
 
 def tile_generatorhead_pb_t_kernel(tc, h_norm, base_w2, spline_w2, out):
@@ -36,13 +39,14 @@ def tile_generatorhead_pb_t_kernel(tc, h_norm, base_w2, spline_w2, out):
     x = h_norm.flatten_outer_dims()
     y = out.flatten_outer_dims()
 
-    with tc.tile_pool(name="const", bufs=1) as const, tc.tile_pool(
-        name="weights", bufs=1
-    ) as weights, tc.tile_pool(name="stage", bufs=2) as stage, tc.tile_pool(
-        name="work", bufs=2
-    ) as work, tc.psum_pool(name="turned", bufs=3) as turned, tc.psum_pool(
-        name="sums", bufs=3
-    ) as sums:
+    with ExitStack() as pools:
+        const = pools.enter_context(tc.tile_pool(name="const", bufs=1))
+        weights = pools.enter_context(tc.tile_pool(name="weights", bufs=1))
+        stage = pools.enter_context(tc.tile_pool(name="stage", bufs=3))
+        work = pools.enter_context(tc.tile_pool(name="work", bufs=PAIRS))
+        turned = pools.enter_context(tc.psum_pool(name="turned", bufs=2))
+        sums = pools.enter_context(tc.psum_pool(name="sums", bufs=3 * TILES))
+
         ident = const.tile([P, P], F32)
         make_identity(nc, ident[:])
 
@@ -53,9 +57,13 @@ def tile_generatorhead_pb_t_kernel(tc, h_norm, base_w2, spline_w2, out):
         nc.vector.tensor_scalar(
             out=outer_bias[:], in0=ones[:], scalar1=-2.0 * k_outer, scalar2=None, op0=ALU.mult
         )
+        mid_bias = const.tile([P, 1], F32)
+        nc.vector.tensor_scalar(
+            out=mid_bias[:], in0=ones[:], scalar1=-2.0 / 3.0, scalar2=None, op0=ALU.mult
+        )
 
         def turn_words(rows_of, grouped):
-            bank = turned.tile([P, 2, HALVES, P], F32, tag="bank")
+            bank = turned.tile([P, 2, HALVES, P], F32)
             for n in range(2):
                 words = rows_of(n).bitcast(F32)
                 for u in range(HALVES):
@@ -65,18 +73,19 @@ def tile_generatorhead_pb_t_kernel(tc, h_norm, base_w2, spline_w2, out):
                 in_=bank[:].rearrange("p n u r -> p n r u"),
             )
 
-        base_raw = weights.tile([P, 2, FEATURES], BF16)
-        nc.sync.dma_start(out=base_raw[:], in_=base_w2.rearrange("(n o) i -> o n i", n=2))
-        spline_raw = weights.tile([P, 2, FEATURES * BASIS], BF16)
-        nc.sync.dma_start(
-            out=spline_raw[:], in_=spline_w2.rearrange("(n o) i c -> o n (i c)", n=2)
-        )
-        spline_by_c = weights.tile([P, 2, BASIS, FEATURES], BF16)
-        for n in range(2):
-            nc.vector.tensor_copy(
-                out=spline_by_c[:, n, :, :],
-                in_=spline_raw[:, n, :].rearrange("o (i c) -> o c i", c=BASIS),
+        def group_tokens(k):
+            x_raw = stage.tile([P, TILES, FEATURES], BF16)
+            nc.sync.dma_start(
+                out=x_raw[:],
+                in_=x[k * CHUNK : (k + 1) * CHUNK, :].rearrange("(p j) i -> p j i", j=TILES),
             )
+            x_grouped = stage.tile([P, CHUNK, PACK], BF16)
+            for j in range(0, TILES, 2):
+                turn_words(
+                    lambda n, j=j: x_raw[:, j + n, :], x_grouped[:, j * P : (j + 2) * P, :]
+                )
+            return x_grouped
+
         w_codes = weights.tile([P, PASSES, OUTPUTS], U32, align_bytes=64)
         w_scales = weights.tile([P, PASSES, OUTPUTS], U8, align_bytes=64)
 
@@ -89,30 +98,29 @@ def tile_generatorhead_pb_t_kernel(tc, h_norm, base_w2, spline_w2, out):
                 in_=w_grouped[:].rearrange("p o t -> p (o t)"),
             )
 
-        quantise_weight(0, lambda n: base_raw[:, n, :])
-        for c in range(BASIS):
-            quantise_weight(pass_of(c), lambda n, c=c: spline_by_c[:, n, c, :])
-
-        for first in range(0, TOKENS, CHUNK):
-            x_raw = stage.tile([P, TILES, FEATURES], BF16)
-            nc.sync.dma_start(
-                out=x_raw[:], in_=x[first : first + CHUNK, :].rearrange("(p j) i -> p j i", j=TILES)
+        def prepare_weights():
+            base_raw = weights.tile([P, 2, FEATURES], BF16)
+            nc.sync.dma_start(out=base_raw[:], in_=base_w2.rearrange("(n o) i -> o n i", n=2))
+            spline_raw = weights.tile([P, 2, FEATURES * BASIS], BF16)
+            nc.scalar.dma_start(
+                out=spline_raw[:], in_=spline_w2.rearrange("(n o) i c -> o n (i c)", n=2)
             )
-            x_grouped = stage.tile([P, CHUNK, PACK], BF16)
-            for j in range(0, TILES, 2):
-                turn_words(
-                    lambda n, j=j: x_raw[:, j + n, :], x_grouped[:, j * P : (j + 2) * P, :]
+            spline_by_c = weights.tile([P, 2, BASIS, FEATURES], BF16)
+            for n in range(2):
+                nc.vector.tensor_copy(
+                    out=spline_by_c[:, n, :, :],
+                    in_=spline_raw[:, n, :].rearrange("o (i c) -> o c i", c=BASIS),
                 )
-            xt = x_grouped[:].rearrange("p s t -> p (s t)")
+            for c in range(BASIS):
+                quantise_weight(pass_of(c), lambda n, c=c: spline_by_c[:, n, c, :])
+            quantise_weight(SILU_PASS, lambda n: base_raw[:, n, :])
 
+        x_grouped = group_tokens(0)
+        prepare_weights()
+        for k in range(CHUNKS):
+            xt = x_grouped[:].rearrange("p s t -> p (s t)")
             codes = stage.tile([P, PASSES, CHUNK], U32, align_bytes=64)
             scales = stage.tile([P, PASSES, CHUNK], U8, align_bytes=64)
-
-            silu = work.tile([P, COLS], BF16, align_bytes=64)
-            nc.scalar.activation(out=silu[:], in_=xt, func=ACT.Silu)
-            nc.vector.quantize_mx(
-                out=codes[:, 0, :].bitcast(FP8X4), scales=scales[:, 0, :], in_=silu[:]
-            )
 
             for r in range(PAIRS):
                 dist = work.tile([P, COLS], F32)
@@ -134,10 +142,16 @@ def tile_generatorhead_pb_t_kernel(tc, h_norm, base_w2, spline_w2, out):
                     op0=ALU.subtract, op1=ALU.mult,
                 )
                 neg_mid = work.tile([P, COLS], BF16)
-                nc.vector.tensor_scalar(
-                    out=neg_mid[:], in0=sq_mid[:], scalar1=-1.0, scalar2=-2.0 / 3.0,
-                    op0=ALU.mult, op1=ALU.add,
-                )
+                if r < PAIRS - 1:
+                    nc.vector.tensor_scalar(
+                        out=neg_mid[:], in0=sq_mid[:], scalar1=-1.0, scalar2=-2.0 / 3.0,
+                        op0=ALU.mult, op1=ALU.add,
+                    )
+                else:
+                    nc.scalar.activation(
+                        out=neg_mid[:], in_=sq_mid[:], func=ACT.Identity, scale=-1.0,
+                        bias=mid_bias[:],
+                    )
                 neg_out = work.tile([P, COLS], BF16)
                 nc.vector.scalar_tensor_tensor(
                     out=neg_out[:], in0=dist[:], scalar=2.0, in1=sq_out[:],
@@ -167,13 +181,22 @@ def tile_generatorhead_pb_t_kernel(tc, h_norm, base_w2, spline_w2, out):
                     in_=pair[:].rearrange("p h f -> p (h f)"),
                 )
 
-            result = stage.tile([P, TILES, OUTPUTS], F32)
-            for j in range(TILES):
-                slots = slice(j * P, (j + 1) * P)
-                acc = sums.tile([P, OUTPUTS], F32)
-                for q in range(PASSES):
+            silu = work.tile([P, COLS], BF16, align_bytes=64)
+            nc.scalar.activation(out=silu[:], in_=xt, func=ACT.Silu)
+            nc.vector.quantize_mx(
+                out=codes[:, SILU_PASS, :].bitcast(FP8X4),
+                scales=scales[:, SILU_PASS, :],
+                in_=silu[:],
+            )
+            if k + 1 < CHUNKS:
+                x_grouped = group_tokens(k + 1)
+
+            accs = [sums.tile([P, OUTPUTS], F32, name="acc") for j in range(TILES)]
+            for q in range(PASSES):
+                for j in range(TILES):
+                    slots = slice(j * P, (j + 1) * P)
                     nc.tensor.matmul_mx(
-                        out=acc[:],
+                        out=accs[j][:],
                         lhsT=codes[:, q, slots].bitcast(FP8X4),
                         lhsT_scale=scales[:, q, slots],
                         rhs=w_codes[:, q, :].bitcast(FP8X4),
@@ -181,8 +204,10 @@ def tile_generatorhead_pb_t_kernel(tc, h_norm, base_w2, spline_w2, out):
                         start=(q == 0),
                         stop=(q == PASSES - 1),
                     )
-                nc.scalar.copy(out=result[:, j, :], in_=acc[:])
+            result = stage.tile([P, TILES, OUTPUTS], F32)
+            for j in range(TILES):
+                nc.scalar.copy(out=result[:, j, :], in_=accs[j][:])
             nc.sync.dma_start(
-                out=y[first : first + CHUNK, :].rearrange("(p j) o -> p j o", j=TILES),
+                out=y[k * CHUNK : (k + 1) * CHUNK, :].rearrange("(p j) o -> p j o", j=TILES),
                 in_=result[:],
             )

@@ -21,17 +21,11 @@ BASIS = 8
 PAIRS = BASIS // 2
 PASSES = BASIS + 1
 SILU_PASS = BASIS
-TILES = 2
-CHUNK = TILES * P
-CHUNKS = TOKENS // CHUNK
-COLS = CHUNK * PACK
+MAX_TILES = 2
 HALVES = 2
+CHUNKS = [1] + [2] * 15 + [1]
 
 FLOPS = 2 * TOKENS * OUTPUTS * FEATURES * PASSES
-
-
-def pass_of(c):
-    return 2 * (c % PAIRS) + c // PAIRS
 
 
 def tile_generatorhead_pb_t_kernel(tc, h_norm, base_w2, spline_w2, out):
@@ -42,10 +36,13 @@ def tile_generatorhead_pb_t_kernel(tc, h_norm, base_w2, spline_w2, out):
     with ExitStack() as pools:
         const = pools.enter_context(tc.tile_pool(name="const", bufs=1))
         weights = pools.enter_context(tc.tile_pool(name="weights", bufs=1))
-        stage = pools.enter_context(tc.tile_pool(name="stage", bufs=3))
-        work = pools.enter_context(tc.tile_pool(name="work", bufs=PAIRS))
+        stage = pools.enter_context(tc.tile_pool(name="stage", bufs=2))
+        work = pools.enter_context(tc.tile_pool(name="work", bufs=2))
+        local = pools.enter_context(tc.tile_pool(name="local", bufs=1))
+        loads = pools.enter_context(tc.tile_pool(name="loads", bufs=3))
         turned = pools.enter_context(tc.psum_pool(name="turned", bufs=2))
-        sums = pools.enter_context(tc.psum_pool(name="sums", bufs=3 * TILES))
+        w_turned = pools.enter_context(tc.psum_pool(name="w_turned", bufs=2))
+        sums = pools.enter_context(tc.psum_pool(name="sums", bufs=2 * MAX_TILES))
 
         ident = const.tile([P, P], F32)
         make_identity(nc, ident[:])
@@ -57,143 +54,131 @@ def tile_generatorhead_pb_t_kernel(tc, h_norm, base_w2, spline_w2, out):
         nc.vector.tensor_scalar(
             out=outer_bias[:], in0=ones[:], scalar1=-2.0 * k_outer, scalar2=None, op0=ALU.mult
         )
-        mid_bias = const.tile([P, 1], F32)
-        nc.vector.tensor_scalar(
-            out=mid_bias[:], in0=ones[:], scalar1=-2.0 / 3.0, scalar2=None, op0=ALU.mult
-        )
 
-        def turn_words(rows_of, grouped):
-            bank = turned.tile([P, 2, HALVES, P], F32)
-            for n in range(2):
-                words = rows_of(n).bitcast(F32)
+        def turn_words(pool, rows):
+            bank = pool.tile([P, 2, HALVES, P], F32, name="bank")
+            for n in range(len(rows)):
+                words = rows[n].bitcast(F32)
                 for u in range(HALVES):
                     nc.tensor.transpose(bank[:, n, u, :], words[:, u * P : (u + 1) * P], ident[:])
-            nc.scalar.copy(
-                out=grouped.bitcast(F32).rearrange("p (n r) u -> p n r u", n=2),
-                in_=bank[:].rearrange("p n u r -> p n r u"),
+            return bank
+
+        def regroup(copy, bank, count, grouped):
+            copy(
+                out=grouped.bitcast(F32).rearrange("p (n r) u -> p n r u", n=count),
+                in_=bank[:, 0:count, :, :].rearrange("p n u r -> p n r u"),
             )
 
-        def group_tokens(k):
-            x_raw = stage.tile([P, TILES, FEATURES], BF16)
+        starts = [sum(CHUNKS[:k]) * P for k in range(len(CHUNKS))]
+
+        def load_tokens(k):
+            tiles = CHUNKS[k]
+            x_raw = loads.tile([P, tiles, FEATURES], BF16, name="x_raw")
             nc.sync.dma_start(
                 out=x_raw[:],
-                in_=x[k * CHUNK : (k + 1) * CHUNK, :].rearrange("(p j) i -> p j i", j=TILES),
+                in_=x[starts[k] : starts[k] + tiles * P, :].rearrange("(p j) i -> p j i", j=tiles),
             )
-            x_grouped = stage.tile([P, CHUNK, PACK], BF16)
-            for j in range(0, TILES, 2):
-                turn_words(
-                    lambda n, j=j: x_raw[:, j + n, :], x_grouped[:, j * P : (j + 2) * P, :]
-                )
-            return x_grouped
+            return x_raw
+
+        def turn_tokens(k, x_raw):
+            return turn_words(turned, [x_raw[:, j, :] for j in range(CHUNKS[k])])
+
+        def regroup_tokens(k, bank):
+            x_grouped = stage.tile([P, CHUNKS[k] * P, PACK], BF16, name="x_grouped")
+            regroup(nc.scalar.copy, bank, CHUNKS[k], x_grouped[:])
+            return x_grouped[:].rearrange("p s t -> p (s t)")
 
         w_codes = weights.tile([P, PASSES, OUTPUTS], U32, align_bytes=64)
         w_scales = weights.tile([P, PASSES, OUTPUTS], U8, align_bytes=64)
 
-        def quantise_weight(q, rows_of):
-            w_grouped = stage.tile([P, OUTPUTS, PACK], BF16, align_bytes=64)
-            turn_words(rows_of, w_grouped[:])
-            nc.vector.quantize_mx(
-                out=w_codes[:, q, :].bitcast(FP8X4),
-                scales=w_scales[:, q, :],
-                in_=w_grouped[:].rearrange("p o t -> p (o t)"),
-            )
-
-        def prepare_weights():
-            base_raw = weights.tile([P, 2, FEATURES], BF16)
-            nc.sync.dma_start(out=base_raw[:], in_=base_w2.rearrange("(n o) i -> o n i", n=2))
-            spline_raw = weights.tile([P, 2, FEATURES * BASIS], BF16)
-            nc.scalar.dma_start(
-                out=spline_raw[:], in_=spline_w2.rearrange("(n o) i c -> o n (i c)", n=2)
-            )
-            spline_by_c = weights.tile([P, 2, BASIS, FEATURES], BF16)
-            for n in range(2):
-                nc.vector.tensor_copy(
-                    out=spline_by_c[:, n, :, :],
-                    in_=spline_raw[:, n, :].rearrange("o (i c) -> o c i", c=BASIS),
-                )
-            for c in range(BASIS):
-                quantise_weight(pass_of(c), lambda n, c=c: spline_by_c[:, n, c, :])
-            quantise_weight(SILU_PASS, lambda n: base_raw[:, n, :])
-
-        x_grouped = group_tokens(0)
-        prepare_weights()
-        for k in range(CHUNKS):
-            xt = x_grouped[:].rearrange("p s t -> p (s t)")
-            codes = stage.tile([P, PASSES, CHUNK], U32, align_bytes=64)
-            scales = stage.tile([P, PASSES, CHUNK], U8, align_bytes=64)
-
+        def scalar_part(k, xt):
+            cols = CHUNKS[k] * P * PACK
+            dist = work.tile([P, PAIRS, cols], F32, name="dist")
             for r in range(PAIRS):
-                dist = work.tile([P, COLS], F32)
                 nc.scalar.activation(
-                    out=dist[:], in_=xt, func=ACT.Abs, scale=2.5, bias=1.5 - r
+                    out=dist[:, r, :], in_=xt, func=ACT.Abs, scale=2.5, bias=1.5 - r
                 )
-                nc.scalar.activation(out=dist[:], in_=dist[:], func=ACT.Abs, bias=-2.0)
-                sq_mid = work.tile([P, COLS], F32)
-                nc.scalar.activation(
-                    out=sq_mid[:], in_=dist[:], func=ACT.Square, scale=1.0 / math.sqrt(2.0)
-                )
-                sq_out = work.tile([P, COLS], F32)
-                nc.scalar.activation(
-                    out=sq_out[:], in_=dist[:], func=ACT.Square, scale=k_outer, bias=outer_bias[:]
-                )
+            nc.scalar.activation(out=dist[:], in_=dist[:], func=ACT.Abs, bias=-2.0)
+            near = work.tile([P, 2, cols], F32, name="near")
+            nc.scalar.activation(out=near[:], in_=dist[:, 1:3, :], func=ACT.Abs, bias=-1.0)
+            sq_mid = work.tile([P, 2, cols], F32, name="sq_mid")
+            nc.scalar.activation(
+                out=sq_mid[:], in_=near[:], func=ACT.Square, scale=1.0 / math.sqrt(2.0)
+            )
+            sq_out = work.tile([P, PAIRS, cols], F32, name="sq_out")
+            nc.scalar.activation(
+                out=sq_out[:], in_=dist[:], func=ACT.Square, scale=k_outer, bias=outer_bias[:]
+            )
+            silu = work.tile([P, cols], BF16, align_bytes=64, name="silu")
+            nc.scalar.activation(out=silu[:], in_=xt, func=ACT.Silu)
+            return dist, near, sq_mid, sq_out, silu
 
-                nc.vector.scalar_tensor_tensor(
-                    out=sq_mid[:], in0=dist[:], scalar=2.0, in1=sq_mid[:],
-                    op0=ALU.subtract, op1=ALU.mult,
-                )
-                neg_mid = work.tile([P, COLS], BF16)
-                if r < PAIRS - 1:
-                    nc.vector.tensor_scalar(
-                        out=neg_mid[:], in0=sq_mid[:], scalar1=-1.0, scalar2=-2.0 / 3.0,
-                        op0=ALU.mult, op1=ALU.add,
-                    )
-                else:
-                    nc.scalar.activation(
-                        out=neg_mid[:], in_=sq_mid[:], func=ACT.Identity, scale=-1.0,
-                        bias=mid_bias[:],
-                    )
-                neg_out = work.tile([P, COLS], BF16)
-                nc.vector.scalar_tensor_tensor(
-                    out=neg_out[:], in0=dist[:], scalar=2.0, in1=sq_out[:],
-                    op0=ALU.subtract, op1=ALU.mult,
-                )
-                nc.vector.tensor_tensor(out=neg_mid[:], in0=neg_mid[:], in1=neg_out[:], op=ALU.max)
-                nc.vector.tensor_scalar_min(out=neg_mid[:], in0=neg_mid[:], scalar1=0.0)
-                side = work.tile([P, COLS], BF16)
+        def vector_part(k, xt, dist, near, sq_mid, sq_out, silu):
+            size = CHUNKS[k] * P
+            cols = size * PACK
+            codes = stage.tile([P, PASSES, size], U32, align_bytes=64, name="codes")
+            scales = stage.tile([P, PASSES, size], U8, align_bytes=64, name="scales")
+            value = local.tile([P, PAIRS, cols], BF16, name="value")
+            nc.vector.scalar_tensor_tensor(
+                out=value[:], in0=dist[:], scalar=2.0, in1=sq_out[:],
+                op0=ALU.subtract, op1=ALU.mult,
+            )
+            nc.vector.scalar_tensor_tensor(
+                out=sq_mid[:], in0=near[:], scalar=2.0, in1=sq_mid[:],
+                op0=ALU.subtract, op1=ALU.mult,
+            )
+            side = local.tile([P, PAIRS, cols], BF16, name="side")
+
+            def make_side(r):
                 nc.vector.tensor_scalar(
-                    out=side[:], in0=xt, scalar1=-2.2 + 0.4 * (r + PAIRS), scalar2=0.5,
+                    out=side[:, r, :], in0=xt, scalar1=-2.2 + 0.4 * (r + PAIRS), scalar2=0.5,
                     op0=ALU.is_lt, op1=ALU.subtract,
                 )
-                nc.vector.tensor_tensor(out=side[:], in0=neg_mid[:], in1=side[:], op=ALU.mult)
-                pair = work.tile([P, 2, COLS], BF16, align_bytes=64)
-                nc.vector.tensor_scalar(
-                    out=pair[:, 0, :], in0=side[:], scalar1=-2.0, scalar2=0.0,
-                    op0=ALU.mult, op1=ALU.max,
-                )
-                nc.vector.tensor_scalar(
-                    out=pair[:, 1, :], in0=side[:], scalar1=2.0, scalar2=0.0,
-                    op0=ALU.mult, op1=ALU.max,
-                )
-                q = pass_of(r)
-                nc.vector.quantize_mx(
-                    out=codes[:, q : q + 2, :].rearrange("p q s -> p (q s)").bitcast(FP8X4),
-                    scales=scales[:, q : q + 2, :].rearrange("p q s -> p (q s)"),
-                    in_=pair[:].rearrange("p h f -> p (h f)"),
-                )
 
-            silu = work.tile([P, COLS], BF16, align_bytes=64)
-            nc.scalar.activation(out=silu[:], in_=xt, func=ACT.Silu)
+            make_side(0)
+            neg_mid = local.tile([P, 2, cols], BF16, name="neg_mid")
+            nc.vector.tensor_scalar(
+                out=neg_mid[:], in0=sq_mid[:], scalar1=-1.0, scalar2=-2.0 / 3.0,
+                op0=ALU.mult, op1=ALU.add,
+            )
+            make_side(1)
+            for h in range(2):
+                nc.vector.tensor_tensor(
+                    out=value[:, 2 * h : 2 * h + 2, :], in0=value[:, 2 * h : 2 * h + 2, :],
+                    in1=neg_mid[:], op=ALU.max,
+                )
+            make_side(2)
+            make_side(3)
+            nc.vector.tensor_scalar_min(out=value[:], in0=value[:], scalar1=0.0)
             nc.vector.quantize_mx(
                 out=codes[:, SILU_PASS, :].bitcast(FP8X4),
                 scales=scales[:, SILU_PASS, :],
                 in_=silu[:],
             )
-            if k + 1 < CHUNKS:
-                x_grouped = group_tokens(k + 1)
+            nc.vector.tensor_tensor(out=value[:], in0=value[:], in1=side[:], op=ALU.mult)
+            basis = [
+                local.tile([P, PAIRS, cols], BF16, align_bytes=64, name="basis%d" % h)
+                for h in range(2)
+            ]
+            for h in range(2):
+                nc.vector.tensor_scalar(
+                    out=basis[h][:], in0=value[:], scalar1=-2.0 if h == 0 else 2.0, scalar2=0.0,
+                    op0=ALU.mult, op1=ALU.max,
+                )
+            for h in range(2):
+                q = h * PAIRS
+                nc.vector.quantize_mx(
+                    out=codes[:, q : q + PAIRS, :].rearrange("p q s -> p (q s)").bitcast(FP8X4),
+                    scales=scales[:, q : q + PAIRS, :].rearrange("p q s -> p (q s)"),
+                    in_=basis[h][:].rearrange("p r f -> p (r f)"),
+                )
+            return codes, scales
 
-            accs = [sums.tile([P, OUTPUTS], F32, name="acc") for j in range(TILES)]
-            for q in range(PASSES):
-                for j in range(TILES):
+        def multiply(k, codes, scales):
+            accs = [sums.tile([P, OUTPUTS], F32, name="acc") for j in range(CHUNKS[k])]
+            order = [SILU_PASS] + list(range(BASIS))
+            for q in order:
+                for j in range(CHUNKS[k]):
                     slots = slice(j * P, (j + 1) * P)
                     nc.tensor.matmul_mx(
                         out=accs[j][:],
@@ -201,13 +186,71 @@ def tile_generatorhead_pb_t_kernel(tc, h_norm, base_w2, spline_w2, out):
                         lhsT_scale=scales[:, q, slots],
                         rhs=w_codes[:, q, :].bitcast(FP8X4),
                         rhs_scale=w_scales[:, q, :],
-                        start=(q == 0),
-                        stop=(q == PASSES - 1),
+                        start=(q == order[0]),
+                        stop=(q == order[-1]),
                     )
-            result = stage.tile([P, TILES, OUTPUTS], F32)
-            for j in range(TILES):
+            return accs
+
+        def store(k, accs):
+            tiles = CHUNKS[k]
+            result = stage.tile([P, tiles, OUTPUTS], F32, name="result")
+            for j in range(tiles):
                 nc.scalar.copy(out=result[:, j, :], in_=accs[j][:])
             nc.sync.dma_start(
-                out=y[k * CHUNK : (k + 1) * CHUNK, :].rearrange("(p j) o -> p j o", j=TILES),
+                out=y[starts[k] : starts[k] + tiles * P, :].rearrange("(p j) o -> p j o", j=tiles),
                 in_=result[:],
             )
+
+        with tc.manual_schedule():
+            last = len(CHUNKS) - 1
+            raws = {0: load_tokens(0)}
+            spline_raw = weights.tile([P, 2, FEATURES * BASIS], BF16)
+            for n in range(2):
+                nc.scalar.dma_start(
+                    out=spline_raw[:, n, :],
+                    in_=spline_w2[n * P : (n + 1) * P, :, :].rearrange("o i c -> o (i c)"),
+                )
+            base_raw = weights.tile([P, 2, FEATURES], BF16)
+            nc.sync.dma_start(out=base_raw[:], in_=base_w2.rearrange("(n o) i -> o n i", n=2))
+            raws[1] = load_tokens(1)
+
+            xt = regroup_tokens(0, turn_tokens(0, raws[0]))
+            parts = scalar_part(0, xt)
+            bank = turn_tokens(1, raws[1])
+
+            spline_by_c = weights.tile([P, 2, BASIS, FEATURES], BF16)
+            for n in range(2):
+                nc.vector.tensor_copy(
+                    out=spline_by_c[:, n, :, :],
+                    in_=spline_raw[:, n, :].rearrange("o (i c) -> o c i", c=BASIS),
+                )
+            for q in [SILU_PASS] + list(range(BASIS)):
+                w_bank = turn_words(
+                    w_turned,
+                    [base_raw[:, n, :] if q == SILU_PASS else spline_by_c[:, n, q, :] for n in range(2)],
+                )
+                w_grouped = stage.tile([P, OUTPUTS, PACK], BF16, align_bytes=64, name="w_grouped")
+                regroup(nc.scalar.copy if q % 2 == 1 else nc.vector.tensor_copy, w_bank, 2, w_grouped[:])
+                nc.vector.quantize_mx(
+                    out=w_codes[:, q, :].bitcast(FP8X4),
+                    scales=w_scales[:, q, :],
+                    in_=w_grouped[:].rearrange("p o t -> p (o t)"),
+                )
+
+            waiting = []
+            for k in range(len(CHUNKS)):
+                if k + 2 <= last:
+                    raws[k + 2] = load_tokens(k + 2)
+                if k + 1 <= last:
+                    next_xt = regroup_tokens(k + 1, bank)
+                    next_parts = scalar_part(k + 1, next_xt)
+                if k + 2 <= last:
+                    bank = turn_tokens(k + 2, raws[k + 2])
+                if len(waiting) > 0:
+                    store(*waiting.pop(0))
+                codes, scales = vector_part(k, xt, *parts)
+                waiting.append((k, multiply(k, codes, scales)))
+                if k + 1 <= last:
+                    xt, parts = next_xt, next_parts
+            for item in waiting:
+                store(*item)

@@ -39,15 +39,16 @@ def tile_generatorhead_pb_t_kernel(tc, h_norm, base_w2, spline_w2, out):
         stage = pools.enter_context(tc.tile_pool(name="stage", bufs=2))
         work = pools.enter_context(tc.tile_pool(name="work", bufs=2))
         local = pools.enter_context(tc.tile_pool(name="local", bufs=1))
+        between = pools.enter_context(tc.tile_pool(name="between", bufs=2))
         loads = pools.enter_context(tc.tile_pool(name="loads", bufs=3))
         turned = pools.enter_context(tc.psum_pool(name="turned", bufs=2))
         w_turned = pools.enter_context(tc.psum_pool(name="w_turned", bufs=2))
-        sums = pools.enter_context(tc.psum_pool(name="sums", bufs=2 * MAX_TILES))
+        sums = pools.enter_context(tc.psum_pool(name="sums", bufs=3))
 
         ident = const.tile([P, P], F32)
         make_identity(nc, ident[:])
 
-        k_outer = 1.0 / math.sqrt(6.0)
+        k_outer = 1.0 / math.sqrt(3.0)
         ones = const.tile([P, 1], F32)
         nc.vector.memset(ones[:], 1.0)
         outer_bias = const.tile([P, 1], F32)
@@ -91,7 +92,7 @@ def tile_generatorhead_pb_t_kernel(tc, h_norm, base_w2, spline_w2, out):
         w_codes = weights.tile([P, PASSES, OUTPUTS], U32, align_bytes=64)
         w_scales = weights.tile([P, PASSES, OUTPUTS], U8, align_bytes=64)
 
-        def scalar_part(k, xt):
+        def scalar_part(k, xt, between_steps):
             cols = CHUNKS[k] * P * PACK
             dist = work.tile([P, PAIRS, cols], F32, name="dist")
             for r in range(PAIRS):
@@ -99,89 +100,110 @@ def tile_generatorhead_pb_t_kernel(tc, h_norm, base_w2, spline_w2, out):
                     out=dist[:, r, :], in_=xt, func=ACT.Abs, scale=2.5, bias=1.5 - r
                 )
             nc.scalar.activation(out=dist[:], in_=dist[:], func=ACT.Abs, bias=-2.0)
-            near = work.tile([P, 2, cols], F32, name="near")
-            nc.scalar.activation(out=near[:], in_=dist[:, 1:3, :], func=ACT.Abs, bias=-1.0)
-            sq_mid = work.tile([P, 2, cols], F32, name="sq_mid")
-            nc.scalar.activation(
-                out=sq_mid[:], in_=near[:], func=ACT.Square, scale=1.0 / math.sqrt(2.0)
-            )
+            between_steps()
+            near = work.tile([P, cols], F32, name="near")
+            nc.scalar.activation(out=near[:], in_=dist[:, 2, :], func=ACT.Abs, bias=-1.0)
             sq_out = work.tile([P, PAIRS, cols], F32, name="sq_out")
             nc.scalar.activation(
                 out=sq_out[:], in_=dist[:], func=ACT.Square, scale=k_outer, bias=outer_bias[:]
             )
+            nc.scalar.activation(out=near[:], in_=near[:], func=ACT.Abs, bias=-1.0)
             silu = work.tile([P, cols], BF16, align_bytes=64, name="silu")
             nc.scalar.activation(out=silu[:], in_=xt, func=ACT.Silu)
+            sq_mid = work.tile([P, 2, cols], F32, name="sq_mid")
+            nc.scalar.activation(out=sq_mid[:, 0, :], in_=near[:], func=ACT.Square)
+            nc.scalar.activation(out=sq_mid[:, 1, :], in_=near[:], func=ACT.Square, bias=-0.5)
             return dist, near, sq_mid, sq_out, silu
 
-        def vector_part(k, xt, dist, near, sq_mid, sq_out, silu):
+        def first_steps(k, xt, dist, near, sq_mid, sq_out, silu):
             size = CHUNKS[k] * P
             cols = size * PACK
             codes = stage.tile([P, PASSES, size], U32, align_bytes=64, name="codes")
             scales = stage.tile([P, PASSES, size], U8, align_bytes=64, name="scales")
-            value = local.tile([P, PAIRS, cols], BF16, name="value")
-            nc.vector.scalar_tensor_tensor(
-                out=value[:], in0=dist[:], scalar=2.0, in1=sq_out[:],
-                op0=ALU.subtract, op1=ALU.mult,
-            )
-            nc.vector.scalar_tensor_tensor(
-                out=sq_mid[:], in0=near[:], scalar=2.0, in1=sq_mid[:],
-                op0=ALU.subtract, op1=ALU.mult,
-            )
-            side = local.tile([P, PAIRS, cols], BF16, name="side")
+            value = between.tile([P, PAIRS, cols], BF16, name="value")
+            side = between.tile([P, PAIRS, cols], BF16, name="side")
+            neg_mid = local.tile([P, 2, cols], BF16, name="neg_mid")
 
-            def make_side(r):
-                nc.vector.tensor_scalar(
-                    out=side[:, r, :], in0=xt, scalar1=-2.2 + 0.4 * (r + PAIRS), scalar2=0.5,
-                    op0=ALU.is_lt, op1=ALU.subtract,
+            def outer():
+                nc.vector.scalar_tensor_tensor(
+                    out=value[:], in0=dist[:], scalar=2.0, in1=sq_out[:],
+                    op0=ALU.subtract, op1=ALU.mult,
                 )
 
-            make_side(0)
-            neg_mid = local.tile([P, 2, cols], BF16, name="neg_mid")
-            nc.vector.tensor_scalar(
-                out=neg_mid[:], in0=sq_mid[:], scalar1=-1.0, scalar2=-2.0 / 3.0,
-                op0=ALU.mult, op1=ALU.add,
-            )
-            make_side(1)
-            for h in range(2):
+            def middle():
+                nc.vector.scalar_tensor_tensor(
+                    out=sq_mid[:, 0, :], in0=near[:], scalar=2.0, in1=sq_mid[:, 0, :],
+                    op0=ALU.subtract, op1=ALU.mult,
+                )
+
+            def middles():
+                nc.vector.tensor_scalar(
+                    out=neg_mid[:, 0, :], in0=sq_mid[:, 0, :], scalar1=-1.0, scalar2=-4.0 / 3.0,
+                    op0=ALU.mult, op1=ALU.add,
+                )
+                nc.vector.scalar_tensor_tensor(
+                    out=neg_mid[:, 1, :], in0=sq_mid[:, 1, :], scalar=7.0 / 12.0,
+                    in1=sq_mid[:, 0, :], op0=ALU.subtract, op1=ALU.add,
+                )
+
+            def larger(h):
                 nc.vector.tensor_tensor(
                     out=value[:, 2 * h : 2 * h + 2, :], in0=value[:, 2 * h : 2 * h + 2, :],
                     in1=neg_mid[:], op=ALU.max,
                 )
-            make_side(2)
-            make_side(3)
-            nc.vector.tensor_scalar_min(out=value[:], in0=value[:], scalar1=0.0)
-            nc.vector.quantize_mx(
-                out=codes[:, SILU_PASS, :].bitcast(FP8X4),
-                scales=scales[:, SILU_PASS, :],
-                in_=silu[:],
-            )
-            nc.vector.tensor_tensor(out=value[:], in0=value[:], in1=side[:], op=ALU.mult)
+
+            def clip():
+                for r in range(PAIRS):
+                    nc.vector.tensor_scalar(
+                        out=side[:, r, :], in0=xt, scalar1=-2.2 + 0.4 * (r + PAIRS), scalar2=0.5,
+                        op0=ALU.is_lt, op1=ALU.subtract,
+                    )
+                nc.vector.tensor_scalar_min(out=value[:], in0=value[:], scalar1=0.0)
+                nc.vector.quantize_mx(
+                    out=codes[:, SILU_PASS, :].bitcast(FP8X4),
+                    scales=scales[:, SILU_PASS, :],
+                    in_=silu[:],
+                )
+
+            steps = [outer, middle, middles, lambda: larger(0), lambda: larger(1), clip]
+            return steps, (k, codes, scales, value, side)
+
+        def last_steps(k, codes, scales, value, side):
+            cols = CHUNKS[k] * P * PACK
             basis = [
                 local.tile([P, PAIRS, cols], BF16, align_bytes=64, name="basis%d" % h)
                 for h in range(2)
             ]
-            for h in range(2):
+
+            def signs():
+                nc.vector.tensor_tensor(out=value[:], in0=value[:], in1=side[:], op=ALU.mult)
+
+            def half(h):
                 nc.vector.tensor_scalar(
-                    out=basis[h][:], in0=value[:], scalar1=-2.0 if h == 0 else 2.0, scalar2=0.0,
+                    out=basis[h][:], in0=value[:], scalar1=-1.0 if h == 0 else 1.0, scalar2=0.0,
                     op0=ALU.mult, op1=ALU.max,
                 )
-            for h in range(2):
+
+            def quantise(h):
                 q = h * PAIRS
                 nc.vector.quantize_mx(
                     out=codes[:, q : q + PAIRS, :].rearrange("p q s -> p (q s)").bitcast(FP8X4),
                     scales=scales[:, q : q + PAIRS, :].rearrange("p q s -> p (q s)"),
                     in_=basis[h][:].rearrange("p r f -> p (r f)"),
                 )
-            return codes, scales
+
+            return [
+                signs, lambda: half(0), lambda: half(1), lambda: quantise(0), lambda: quantise(1)
+            ]
 
         def multiply(k, codes, scales):
-            accs = [sums.tile([P, OUTPUTS], F32, name="acc") for j in range(CHUNKS[k])]
+            acc = sums.tile([P, CHUNKS[k], OUTPUTS], F32, name="acc")
             order = [SILU_PASS] + list(range(BASIS))
-            for q in order:
-                for j in range(CHUNKS[k]):
+            for j in range(CHUNKS[k]):
+                for q in order:
                     slots = slice(j * P, (j + 1) * P)
                     nc.tensor.matmul_mx(
-                        out=accs[j][:],
+                        out=acc[:, j, :],
                         lhsT=codes[:, q, slots].bitcast(FP8X4),
                         lhsT_scale=scales[:, q, slots],
                         rhs=w_codes[:, q, :].bitcast(FP8X4),
@@ -189,13 +211,12 @@ def tile_generatorhead_pb_t_kernel(tc, h_norm, base_w2, spline_w2, out):
                         start=(q == order[0]),
                         stop=(q == order[-1]),
                     )
-            return accs
+            return acc
 
-        def store(k, accs):
+        def store(k, acc):
             tiles = CHUNKS[k]
             result = stage.tile([P, tiles, OUTPUTS], F32, name="result")
-            for j in range(tiles):
-                nc.scalar.copy(out=result[:, j, :], in_=accs[j][:])
+            nc.scalar.copy(out=result[:], in_=acc[:])
             nc.sync.dma_start(
                 out=y[starts[k] : starts[k] + tiles * P, :].rearrange("(p j) o -> p j o", j=tiles),
                 in_=result[:],
@@ -215,7 +236,7 @@ def tile_generatorhead_pb_t_kernel(tc, h_norm, base_w2, spline_w2, out):
             raws[1] = load_tokens(1)
 
             xt = regroup_tokens(0, turn_tokens(0, raws[0]))
-            parts = scalar_part(0, xt)
+            parts = scalar_part(0, xt, lambda: None)
             bank = turn_tokens(1, raws[1])
 
             spline_by_c = weights.tile([P, 2, BASIS, FEATURES], BF16)
@@ -237,20 +258,35 @@ def tile_generatorhead_pb_t_kernel(tc, h_norm, base_w2, spline_w2, out):
                     in_=w_grouped[:].rearrange("p o t -> p (o t)"),
                 )
 
-            waiting = []
+            before = None
+            older = None
             for k in range(len(CHUNKS)):
                 if k + 2 <= last:
                     raws[k + 2] = load_tokens(k + 2)
                 if k + 1 <= last:
                     next_xt = regroup_tokens(k + 1, bank)
-                    next_parts = scalar_part(k + 1, next_xt)
+                    next_parts = scalar_part(
+                        k + 1, next_xt, lambda: store(k - 2, older) if k >= 2 else None
+                    )
                 if k + 2 <= last:
                     bank = turn_tokens(k + 2, raws[k + 2])
-                if len(waiting) > 0:
-                    store(*waiting.pop(0))
-                codes, scales = vector_part(k, xt, *parts)
-                waiting.append((k, multiply(k, codes, scales)))
+                first, state = first_steps(k, xt, *parts)
+                rest = last_steps(*before) if before else []
+                for i in range(max(len(first), len(rest))):
+                    if i < len(first):
+                        first[i]()
+                    if i < len(rest):
+                        rest[i]()
+                if before:
+                    done = multiply(*before[0:3])
+                    if k == last:
+                        store(k - 2, older)
+                    older = done
+                before = state
                 if k + 1 <= last:
                     xt, parts = next_xt, next_parts
-            for item in waiting:
-                store(*item)
+            for step in last_steps(*before):
+                step()
+            done = multiply(*before[0:3])
+            store(last - 1, older)
+            store(last, done)

@@ -21,9 +21,9 @@ BASIS = 8
 PAIRS = BASIS // 2
 PASSES = BASIS + 1
 SILU_PASS = BASIS
-MAX_TILES = 2
 HALVES = 2
 CHUNKS = [1] + [2] * 15 + [1]
+BANK_TILES = 2
 
 FLOPS = 2 * TOKENS * OUTPUTS * FEATURES * PASSES
 
@@ -35,15 +35,13 @@ def tile_generatorhead_pb_t_kernel(tc, h_norm, base_w2, spline_w2, out):
 
     with ExitStack() as pools:
         const = pools.enter_context(tc.tile_pool(name="const", bufs=1))
-        weights = pools.enter_context(tc.tile_pool(name="weights", bufs=1))
-        stage = pools.enter_context(tc.tile_pool(name="stage", bufs=2))
-        work = pools.enter_context(tc.tile_pool(name="work", bufs=2))
-        local = pools.enter_context(tc.tile_pool(name="local", bufs=1))
-        between = pools.enter_context(tc.tile_pool(name="between", bufs=2))
-        loads = pools.enter_context(tc.tile_pool(name="loads", bufs=3))
+        single = pools.enter_context(tc.tile_pool(name="single", bufs=1))
+        double = pools.enter_context(tc.tile_pool(name="double", bufs=2))
+        squares = pools.enter_context(tc.tile_pool(name="squares", bufs=8))
+        distances = pools.enter_context(tc.tile_pool(name="distances", bufs=8))
         turned = pools.enter_context(tc.psum_pool(name="turned", bufs=2))
         w_turned = pools.enter_context(tc.psum_pool(name="w_turned", bufs=2))
-        sums = pools.enter_context(tc.psum_pool(name="sums", bufs=3))
+        sums = pools.enter_context(tc.psum_pool(name="sums", bufs=4))
 
         ident = const.tile([P, P], F32)
         make_identity(nc, ident[:])
@@ -71,10 +69,16 @@ def tile_generatorhead_pb_t_kernel(tc, h_norm, base_w2, spline_w2, out):
             )
 
         starts = [sum(CHUNKS[:k]) * P for k in range(len(CHUNKS))]
+        last = len(CHUNKS) - 1
+
+        def banks_of(k):
+            return [
+                (j, min(BANK_TILES, CHUNKS[k] - j)) for j in range(0, CHUNKS[k], BANK_TILES)
+            ]
 
         def load_tokens(k):
             tiles = CHUNKS[k]
-            x_raw = loads.tile([P, tiles, FEATURES], BF16, name="x_raw")
+            x_raw = double.tile([P, tiles, FEATURES], BF16, name="x_raw")
             nc.sync.dma_start(
                 out=x_raw[:],
                 in_=x[starts[k] : starts[k] + tiles * P, :].rearrange("(p j) i -> p j i", j=tiles),
@@ -82,164 +86,228 @@ def tile_generatorhead_pb_t_kernel(tc, h_norm, base_w2, spline_w2, out):
             return x_raw
 
         def turn_tokens(k, x_raw):
-            return turn_words(turned, [x_raw[:, j, :] for j in range(CHUNKS[k])])
+            return [
+                turn_words(turned, [x_raw[:, j + n, :] for n in range(count)])
+                for j, count in banks_of(k)
+            ]
 
-        def regroup_tokens(k, bank):
-            x_grouped = stage.tile([P, CHUNKS[k] * P, PACK], BF16, name="x_grouped")
-            regroup(nc.scalar.copy, bank, CHUNKS[k], x_grouped[:])
+        def regroup_tokens(k, banks):
+            x_grouped = double.tile([P, CHUNKS[k] * P, PACK], BF16, name="x_grouped")
+            for bank, (j, count) in zip(banks, banks_of(k)):
+                regroup(nc.scalar.copy, bank, count, x_grouped[:, j * P : (j + count) * P, :])
             return x_grouped[:].rearrange("p s t -> p (s t)")
 
-        w_codes = weights.tile([P, PASSES, OUTPUTS], U32, align_bytes=64)
-        w_scales = weights.tile([P, PASSES, OUTPUTS], U8, align_bytes=64)
+        w_codes = single.tile([P, PASSES, OUTPUTS], U32, align_bytes=64)
+        w_scales = single.tile([P, PASSES, OUTPUTS], U8, align_bytes=64)
 
-        def scalar_part(k, xt, between_steps):
+        def scalar_part(k, xt):
             cols = CHUNKS[k] * P * PACK
-            dist = work.tile([P, PAIRS, cols], F32, name="dist")
-            for r in range(PAIRS):
+            dist = {}
+            square = {}
+
+            def first_fold(r):
+                if r == 2:
+                    dist[r] = double.tile([P, cols], F32, name="dist2")
+                else:
+                    dist[r] = distances.tile([P, cols], F32, name="dist")
                 nc.scalar.activation(
-                    out=dist[:, r, :], in_=xt, func=ACT.Abs, scale=2.5, bias=1.5 - r
+                    out=dist[r][:], in_=xt, func=ACT.Abs, scale=2.5, bias=1.5 - r
                 )
-            nc.scalar.activation(out=dist[:], in_=dist[:], func=ACT.Abs, bias=-2.0)
-            between_steps()
-            near = work.tile([P, cols], F32, name="near")
-            nc.scalar.activation(out=near[:], in_=dist[:, 2, :], func=ACT.Abs, bias=-1.0)
-            sq_out = work.tile([P, PAIRS, cols], F32, name="sq_out")
-            nc.scalar.activation(
-                out=sq_out[:], in_=dist[:], func=ACT.Square, scale=k_outer, bias=outer_bias[:]
-            )
+
+            def second_fold(r):
+                nc.scalar.activation(out=dist[r][:], in_=dist[r][:], func=ACT.Abs, bias=-2.0)
+
+            def outer_square(r):
+                square[r] = squares.tile([P, cols], F32, name="square")
+                nc.scalar.activation(
+                    out=square[r][:], in_=dist[r][:], func=ACT.Square, scale=k_outer,
+                    bias=outer_bias[:],
+                )
+
+            near = double.tile([P, cols], F32, name="near")
+            sq_even = double.tile([P, cols], F32, name="sq_even")
+            sq_both = double.tile([P, cols], F32, name="sq_both")
+            silu = double.tile([P, cols], BF16, align_bytes=64, name="silu")
+            first_fold(2)
+            first_fold(0)
+            second_fold(2)
+            second_fold(0)
+            nc.scalar.activation(out=near[:], in_=dist[2][:], func=ACT.Abs, bias=-1.0)
+            outer_square(0)
             nc.scalar.activation(out=near[:], in_=near[:], func=ACT.Abs, bias=-1.0)
-            silu = work.tile([P, cols], BF16, align_bytes=64, name="silu")
+            first_fold(1)
+            nc.scalar.activation(out=sq_even[:], in_=near[:], func=ACT.Square)
+            second_fold(1)
+            nc.scalar.activation(out=sq_both[:], in_=near[:], func=ACT.Square, bias=-0.5)
+            outer_square(1)
             nc.scalar.activation(out=silu[:], in_=xt, func=ACT.Silu)
-            sq_mid = work.tile([P, 2, cols], F32, name="sq_mid")
-            nc.scalar.activation(out=sq_mid[:, 0, :], in_=near[:], func=ACT.Square)
-            nc.scalar.activation(out=sq_mid[:, 1, :], in_=near[:], func=ACT.Square, bias=-0.5)
-            return dist, near, sq_mid, sq_out, silu
 
-        def first_steps(k, xt, dist, near, sq_mid, sq_out, silu):
-            size = CHUNKS[k] * P
-            cols = size * PACK
-            codes = stage.tile([P, PASSES, size], U32, align_bytes=64, name="codes")
-            scales = stage.tile([P, PASSES, size], U8, align_bytes=64, name="scales")
-            value = between.tile([P, PAIRS, cols], BF16, name="value")
-            side = between.tile([P, PAIRS, cols], BF16, name="side")
-            neg_mid = local.tile([P, 2, cols], BF16, name="neg_mid")
+            def second_half(inserts):
+                first_fold(3)
+                outer_square(2)
+                second_fold(3)
+                for insert in inserts:
+                    insert()
+                outer_square(3)
 
-            def outer():
+            return (dist, square, near, sq_even, sq_both, silu), second_half
+
+        def group_steps(k, g, xt, state, parts):
+            dist, square, near, sq_even, sq_both, silu = parts
+            codes, scales, neg_mid = state
+            cols = CHUNKS[k] * P * PACK
+            value = double.tile([P, 2, cols], BF16, align_bytes=64, name="value")
+            side = single.tile([P, 2, cols], BF16, name="side")
+
+            def outer(h):
+                r = 2 * g + h
                 nc.vector.scalar_tensor_tensor(
-                    out=value[:], in0=dist[:], scalar=2.0, in1=sq_out[:],
+                    out=value[:, h, :], in0=dist[r][:], scalar=2.0, in1=square[r][:],
                     op0=ALU.subtract, op1=ALU.mult,
                 )
 
             def middle():
                 nc.vector.scalar_tensor_tensor(
-                    out=sq_mid[:, 0, :], in0=near[:], scalar=2.0, in1=sq_mid[:, 0, :],
+                    out=sq_even[:], in0=near[:], scalar=2.0, in1=sq_even[:],
                     op0=ALU.subtract, op1=ALU.mult,
                 )
 
-            def middles():
+            def middle_even():
                 nc.vector.tensor_scalar(
-                    out=neg_mid[:, 0, :], in0=sq_mid[:, 0, :], scalar1=-1.0, scalar2=-4.0 / 3.0,
+                    out=neg_mid[:, 0, :], in0=sq_even[:], scalar1=-1.0, scalar2=-4.0 / 3.0,
                     op0=ALU.mult, op1=ALU.add,
                 )
+
+            def middle_odd():
                 nc.vector.scalar_tensor_tensor(
-                    out=neg_mid[:, 1, :], in0=sq_mid[:, 1, :], scalar=7.0 / 12.0,
-                    in1=sq_mid[:, 0, :], op0=ALU.subtract, op1=ALU.add,
+                    out=neg_mid[:, 1, :], in0=sq_both[:], scalar=7.0 / 12.0, in1=sq_even[:],
+                    op0=ALU.subtract, op1=ALU.add,
                 )
 
-            def larger(h):
-                nc.vector.tensor_tensor(
-                    out=value[:, 2 * h : 2 * h + 2, :], in0=value[:, 2 * h : 2 * h + 2, :],
-                    in1=neg_mid[:], op=ALU.max,
-                )
-
-            def clip():
-                for r in range(PAIRS):
+            def sides():
+                for h in range(2):
                     nc.vector.tensor_scalar(
-                        out=side[:, r, :], in0=xt, scalar1=-2.2 + 0.4 * (r + PAIRS), scalar2=0.5,
-                        op0=ALU.is_lt, op1=ALU.subtract,
+                        out=side[:, h, :], in0=xt, scalar1=-2.2 + 0.4 * (2 * g + h + PAIRS),
+                        scalar2=0.5, op0=ALU.is_lt, op1=ALU.subtract,
                     )
-                nc.vector.tensor_scalar_min(out=value[:], in0=value[:], scalar1=0.0)
+
+            def larger():
+                nc.vector.tensor_tensor(out=value[:], in0=value[:], in1=neg_mid[:], op=ALU.max)
+
+            def quantise_silu():
                 nc.vector.quantize_mx(
                     out=codes[:, SILU_PASS, :].bitcast(FP8X4),
                     scales=scales[:, SILU_PASS, :],
                     in_=silu[:],
                 )
 
-            steps = [outer, middle, middles, lambda: larger(0), lambda: larger(1), clip]
-            return steps, (k, codes, scales, value, side)
+            def clip():
+                nc.vector.tensor_scalar_min(out=value[:], in0=value[:], scalar1=0.0)
 
-        def last_steps(k, codes, scales, value, side):
-            cols = CHUNKS[k] * P * PACK
+            front = [lambda: outer(0), lambda: outer(1)]
+            if g == 0:
+                front += [middle, middle_even, middle_odd, sides, larger, quantise_silu, clip]
+            else:
+                front += [sides, larger, clip]
+
             basis = [
-                local.tile([P, PAIRS, cols], BF16, align_bytes=64, name="basis%d" % h)
-                for h in range(2)
+                single.tile([P, 2, cols], BF16, align_bytes=64, name="basis%d" % s)
+                for s in range(2)
             ]
 
             def signs():
                 nc.vector.tensor_tensor(out=value[:], in0=value[:], in1=side[:], op=ALU.mult)
 
-            def half(h):
+            def split(s):
                 nc.vector.tensor_scalar(
-                    out=basis[h][:], in0=value[:], scalar1=-1.0 if h == 0 else 1.0, scalar2=0.0,
+                    out=basis[s][:], in0=value[:], scalar1=-1.0 if s == 0 else 1.0, scalar2=0.0,
                     op0=ALU.mult, op1=ALU.max,
                 )
 
-            def quantise(h):
-                q = h * PAIRS
+            def quantise(s):
+                q = s * PAIRS + 2 * g
                 nc.vector.quantize_mx(
-                    out=codes[:, q : q + PAIRS, :].rearrange("p q s -> p (q s)").bitcast(FP8X4),
-                    scales=scales[:, q : q + PAIRS, :].rearrange("p q s -> p (q s)"),
-                    in_=basis[h][:].rearrange("p r f -> p (r f)"),
+                    out=codes[:, q : q + 2, :].rearrange("p q s -> p (q s)").bitcast(FP8X4),
+                    scales=scales[:, q : q + 2, :].rearrange("p q s -> p (q s)"),
+                    in_=basis[s][:].rearrange("p h f -> p (h f)"),
                 )
 
-            return [
-                signs, lambda: half(0), lambda: half(1), lambda: quantise(0), lambda: quantise(1)
+            back = [
+                signs, lambda: split(0), lambda: split(1), lambda: quantise(0), lambda: quantise(1)
             ]
+            return front, back
+
+        def weave(first, second):
+            for i in range(max(len(first), len(second))):
+                if i < len(first):
+                    first[i]()
+                if i < len(second):
+                    second[i]()
 
         def multiply(k, codes, scales):
-            acc = sums.tile([P, CHUNKS[k], OUTPUTS], F32, name="acc")
+            accs = []
             order = [SILU_PASS] + list(range(BASIS))
-            for j in range(CHUNKS[k]):
-                for q in order:
+            for start_tile, count in banks_of(k):
+                acc = sums.tile([P, count, OUTPUTS], F32, name="acc")
+                for n in range(count):
+                    j = start_tile + n
                     slots = slice(j * P, (j + 1) * P)
-                    nc.tensor.matmul_mx(
-                        out=acc[:, j, :],
-                        lhsT=codes[:, q, slots].bitcast(FP8X4),
-                        lhsT_scale=scales[:, q, slots],
-                        rhs=w_codes[:, q, :].bitcast(FP8X4),
-                        rhs_scale=w_scales[:, q, :],
-                        start=(q == order[0]),
-                        stop=(q == order[-1]),
-                    )
-            return acc
+                    for q in order:
+                        nc.tensor.matmul_mx(
+                            out=acc[:, n, :],
+                            lhsT=codes[:, q, slots].bitcast(FP8X4),
+                            lhsT_scale=scales[:, q, slots],
+                            rhs=w_codes[:, q, :].bitcast(FP8X4),
+                            rhs_scale=w_scales[:, q, :],
+                            start=(q == order[0]),
+                            stop=(q == order[-1]),
+                        )
+                accs.append(acc)
+            return accs
 
-        def store(k, acc):
+        def store_steps(k, accs):
             tiles = CHUNKS[k]
-            result = stage.tile([P, tiles, OUTPUTS], F32, name="result")
-            nc.scalar.copy(out=result[:], in_=acc[:])
-            nc.sync.dma_start(
-                out=y[starts[k] : starts[k] + tiles * P, :].rearrange("(p j) o -> p j o", j=tiles),
-                in_=result[:],
-            )
+            result = single.tile([P, tiles, OUTPUTS], F32, name="result")
+
+            def copy_out(b, copy):
+                j, count = banks_of(k)[b]
+                copy(out=result[:, j : j + count, :], in_=accs[b][:])
+
+            def send():
+                nc.sync.dma_start(
+                    out=y[starts[k] : starts[k] + tiles * P, :].rearrange(
+                        "(p j) o -> p j o", j=tiles
+                    ),
+                    in_=result[:],
+                )
+
+            return copy_out, send
 
         with tc.manual_schedule():
-            last = len(CHUNKS) - 1
             raws = {0: load_tokens(0)}
-            spline_raw = weights.tile([P, 2, FEATURES * BASIS], BF16)
+            spline_raw = double.tile([P, 2, FEATURES * BASIS], BF16, align_bytes=64, name="codes")
             for n in range(2):
                 nc.scalar.dma_start(
                     out=spline_raw[:, n, :],
                     in_=spline_w2[n * P : (n + 1) * P, :, :].rearrange("o i c -> o (i c)"),
                 )
-            base_raw = weights.tile([P, 2, FEATURES], BF16)
+            base_raw = const.tile([P, 2, FEATURES], BF16)
             nc.sync.dma_start(out=base_raw[:], in_=base_w2.rearrange("(n o) i -> o n i", n=2))
             raws[1] = load_tokens(1)
 
             xt = regroup_tokens(0, turn_tokens(0, raws[0]))
-            parts = scalar_part(0, xt, lambda: None)
-            bank = turn_tokens(1, raws[1])
+            banks = turn_tokens(1, raws[1])
+            xts = {0: xt}
 
-            spline_by_c = weights.tile([P, 2, BASIS, FEATURES], BF16)
+            def regroup_next(k, banks):
+                xts[k] = regroup_tokens(k, banks)
+
+            parts, second_half = scalar_part(0, xts[0])
+            second_half([lambda: regroup_next(1, banks)])
+
+            spline_by_c = double.tile(
+                [P, 2, BASIS, FEATURES], BF16, align_bytes=64, name="codes"
+            )
             for n in range(2):
                 nc.vector.tensor_copy(
                     out=spline_by_c[:, n, :, :],
@@ -250,43 +318,54 @@ def tile_generatorhead_pb_t_kernel(tc, h_norm, base_w2, spline_w2, out):
                     w_turned,
                     [base_raw[:, n, :] if q == SILU_PASS else spline_by_c[:, n, q, :] for n in range(2)],
                 )
-                w_grouped = stage.tile([P, OUTPUTS, PACK], BF16, align_bytes=64, name="w_grouped")
-                regroup(nc.scalar.copy if q % 2 == 1 else nc.vector.tensor_copy, w_bank, 2, w_grouped[:])
+                w_grouped = double.tile([P, OUTPUTS, PACK], BF16, align_bytes=64, name="value")
+                regroup(nc.vector.tensor_copy, w_bank, 2, w_grouped[:])
                 nc.vector.quantize_mx(
                     out=w_codes[:, q, :].bitcast(FP8X4),
                     scales=w_scales[:, q, :],
                     in_=w_grouped[:].rearrange("p o t -> p (o t)"),
                 )
 
-            before = None
-            older = None
+            back = []
+            finished = None
             for k in range(len(CHUNKS)):
+                size = CHUNKS[k] * P
+                codes = double.tile([P, PASSES, size], U32, align_bytes=64, name="codes")
+                scales = double.tile([P, PASSES, size], U8, align_bytes=64, name="scales")
+                neg_mid = single.tile([P, 2, size * PACK], BF16, name="neg_mid")
+                state = (codes, scales, neg_mid)
+
+                front, next_back = group_steps(k, 0, xts[k], state, parts)
+                weave(front, back)
+                if k > 0:
+                    finished = multiply(k - 1, *before)
+                back = next_back
                 if k + 2 <= last:
-                    raws[k + 2] = load_tokens(k + 2)
-                if k + 1 <= last:
-                    next_xt = regroup_tokens(k + 1, bank)
-                    next_parts = scalar_part(
-                        k + 1, next_xt, lambda: store(k - 2, older) if k >= 2 else None
-                    )
+                    banks = turn_tokens(k + 2, load_tokens(k + 2))
+                if k < last:
+                    next_parts, second_half = scalar_part(k + 1, xts[k + 1])
+
+                front, next_back = group_steps(k, 1, xts[k], state, parts)
+                weave(front, back)
+                back = next_back
+                inserts = []
+                if k > 0:
+                    copy_out, send = store_steps(k - 1, finished)
+                    for b in range(len(banks_of(k - 1))):
+                        inserts.append(lambda b=b, f=copy_out: f(b, nc.vector.tensor_copy))
+                    inserts.append(send)
                 if k + 2 <= last:
-                    bank = turn_tokens(k + 2, raws[k + 2])
-                first, state = first_steps(k, xt, *parts)
-                rest = last_steps(*before) if before else []
-                for i in range(max(len(first), len(rest))):
-                    if i < len(first):
-                        first[i]()
-                    if i < len(rest):
-                        rest[i]()
-                if before:
-                    done = multiply(*before[0:3])
-                    if k == last:
-                        store(k - 2, older)
-                    older = done
-                before = state
-                if k + 1 <= last:
-                    xt, parts = next_xt, next_parts
-            for step in last_steps(*before):
+                    inserts.append(lambda k=k, banks=banks: regroup_next(k + 2, banks))
+                if k < last:
+                    second_half(inserts)
+                    parts = next_parts
+                else:
+                    for insert in inserts:
+                        insert()
+                before = (codes, scales)
+            for step in back:
                 step()
-            done = multiply(*before[0:3])
-            store(last - 1, older)
-            store(last, done)
+            copy_out, send = store_steps(last, multiply(last, *before))
+            for b in range(len(banks_of(last))):
+                copy_out(b, nc.scalar.copy)
+            send()

@@ -37,8 +37,7 @@ def tile_generatorhead_pb_t_kernel(tc, h_norm, base_w2, spline_w2, out):
         const = pools.enter_context(tc.tile_pool(name="const", bufs=1))
         single = pools.enter_context(tc.tile_pool(name="single", bufs=1))
         double = pools.enter_context(tc.tile_pool(name="double", bufs=2))
-        squares = pools.enter_context(tc.tile_pool(name="squares", bufs=8))
-        distances = pools.enter_context(tc.tile_pool(name="distances", bufs=8))
+        triple = pools.enter_context(tc.tile_pool(name="triple", bufs=3))
         turned = pools.enter_context(tc.psum_pool(name="turned", bufs=2))
         w_turned = pools.enter_context(tc.psum_pool(name="w_turned", bufs=2))
         sums = pools.enter_context(tc.psum_pool(name="sums", bufs=4))
@@ -92,7 +91,7 @@ def tile_generatorhead_pb_t_kernel(tc, h_norm, base_w2, spline_w2, out):
             ]
 
         def regroup_tokens(k, banks):
-            x_grouped = double.tile([P, CHUNKS[k] * P, PACK], BF16, name="x_grouped")
+            x_grouped = triple.tile([P, CHUNKS[k] * P, PACK], BF16, name="x_grouped")
             for bank, (j, count) in zip(banks, banks_of(k)):
                 regroup(nc.scalar.copy, bank, count, x_grouped[:, j * P : (j + count) * P, :])
             return x_grouped[:].rearrange("p s t -> p (s t)")
@@ -100,99 +99,98 @@ def tile_generatorhead_pb_t_kernel(tc, h_norm, base_w2, spline_w2, out):
         w_codes = single.tile([P, PASSES, OUTPUTS], U32, align_bytes=64)
         w_scales = single.tile([P, PASSES, OUTPUTS], U8, align_bytes=64)
 
-        def scalar_part(k, xt):
+        def scalar_part(k, xt, insert):
             cols = CHUNKS[k] * P * PACK
-            dist = {}
-            square = {}
+            dist = [triple.tile([P, 2, cols], F32, name="dist%d" % g) for g in range(2)]
+            square = [double.tile([P, 2, cols], F32, name="square%d" % g) for g in range(2)]
+            near = double.tile([P, cols], F32, name="near")
+            sq_odd = double.tile([P, cols], F32, name="sq_odd")
+            sq_both = double.tile([P, cols], F32, name="sq_both")
+            silu = double.tile([P, cols], BF16, align_bytes=64, name="silu")
 
             def first_fold(r):
-                if r == 2:
-                    dist[r] = double.tile([P, cols], F32, name="dist2")
-                else:
-                    dist[r] = distances.tile([P, cols], F32, name="dist")
                 nc.scalar.activation(
-                    out=dist[r][:], in_=xt, func=ACT.Abs, scale=2.5, bias=1.5 - r
+                    out=dist[r // 2][:, r % 2, :], in_=xt, func=ACT.Abs, scale=2.5, bias=1.5 - r
                 )
 
-            def second_fold(r):
-                nc.scalar.activation(out=dist[r][:], in_=dist[r][:], func=ACT.Abs, bias=-2.0)
+            def second_fold(g):
+                nc.scalar.activation(out=dist[g][:], in_=dist[g][:], func=ACT.Abs, bias=-2.0)
 
-            def outer_square(r):
-                square[r] = squares.tile([P, cols], F32, name="square")
+            def outer_square(g):
                 nc.scalar.activation(
-                    out=square[r][:], in_=dist[r][:], func=ACT.Square, scale=k_outer,
+                    out=square[g][:], in_=dist[g][:], func=ACT.Square, scale=k_outer,
                     bias=outer_bias[:],
                 )
 
-            near = double.tile([P, cols], F32, name="near")
-            sq_even = double.tile([P, cols], F32, name="sq_even")
-            sq_both = double.tile([P, cols], F32, name="sq_both")
-            silu = double.tile([P, cols], BF16, align_bytes=64, name="silu")
-            first_fold(2)
+            first_fold(1)
             first_fold(0)
-            second_fold(2)
+            first_fold(2)
             second_fold(0)
-            nc.scalar.activation(out=near[:], in_=dist[2][:], func=ACT.Abs, bias=-1.0)
+            first_fold(3)
+            nc.scalar.activation(out=near[:], in_=dist[0][:, 1, :], func=ACT.Abs, bias=-1.0)
             outer_square(0)
             nc.scalar.activation(out=near[:], in_=near[:], func=ACT.Abs, bias=-1.0)
-            first_fold(1)
-            nc.scalar.activation(out=sq_even[:], in_=near[:], func=ACT.Square)
             second_fold(1)
-            nc.scalar.activation(out=sq_both[:], in_=near[:], func=ACT.Square, bias=-0.5)
-            outer_square(1)
+            nc.scalar.activation(out=sq_odd[:], in_=near[:], func=ACT.Square)
             nc.scalar.activation(out=silu[:], in_=xt, func=ACT.Silu)
+            nc.scalar.activation(out=sq_both[:], in_=near[:], func=ACT.Square, bias=-0.5)
+            insert()
+            outer_square(1)
+            return dist, square, near, sq_odd, sq_both, silu
 
-            def second_half(inserts):
-                first_fold(3)
-                outer_square(2)
-                second_fold(3)
-                for insert in inserts:
-                    insert()
-                outer_square(3)
+        def vector_steps(k, xt, parts):
+            dist, square, near, sq_odd, sq_both, silu = parts
+            size = CHUNKS[k] * P
+            cols = size * PACK
+            codes = double.tile([P, PASSES, size], U32, align_bytes=64, name="codes")
+            scales = double.tile([P, PASSES, size], U8, align_bytes=64, name="scales")
+            neg_mid = single.tile([P, 2, cols], BF16, name="neg_mid")
+            value = double.tile([P, PAIRS, cols], BF16, align_bytes=64, name="value")
+            side = single.tile([P, PAIRS, cols], BF16, name="side")
+            basis = [
+                single.tile([P, PAIRS, cols], BF16, align_bytes=64, name="basis%d" % s)
+                for s in range(2)
+            ]
 
-            return (dist, square, near, sq_even, sq_both, silu), second_half
-
-        def group_steps(k, g, xt, state, parts):
-            dist, square, near, sq_even, sq_both, silu = parts
-            codes, scales, neg_mid = state
-            cols = CHUNKS[k] * P * PACK
-            value = double.tile([P, 2, cols], BF16, align_bytes=64, name="value")
-            side = single.tile([P, 2, cols], BF16, name="side")
-
-            def outer(h):
-                r = 2 * g + h
+            def outer(g):
                 nc.vector.scalar_tensor_tensor(
-                    out=value[:, h, :], in0=dist[r][:], scalar=2.0, in1=square[r][:],
-                    op0=ALU.subtract, op1=ALU.mult,
+                    out=value[:, 2 * g : 2 * g + 2, :], in0=dist[g][:], scalar=2.0,
+                    in1=square[g][:], op0=ALU.subtract, op1=ALU.mult,
                 )
 
             def middle():
                 nc.vector.scalar_tensor_tensor(
-                    out=sq_even[:], in0=near[:], scalar=2.0, in1=sq_even[:],
+                    out=sq_odd[:], in0=near[:], scalar=2.0, in1=sq_odd[:],
                     op0=ALU.subtract, op1=ALU.mult,
                 )
 
-            def middle_even():
+            def middle_odd():
                 nc.vector.tensor_scalar(
-                    out=neg_mid[:, 0, :], in0=sq_even[:], scalar1=-1.0, scalar2=-4.0 / 3.0,
+                    out=neg_mid[:, 1, :], in0=sq_odd[:], scalar1=-1.0, scalar2=-4.0 / 3.0,
                     op0=ALU.mult, op1=ALU.add,
                 )
 
-            def middle_odd():
+            def middle_even():
                 nc.vector.scalar_tensor_tensor(
-                    out=neg_mid[:, 1, :], in0=sq_both[:], scalar=7.0 / 12.0, in1=sq_even[:],
+                    out=neg_mid[:, 0, :], in0=sq_both[:], scalar=7.0 / 12.0, in1=sq_odd[:],
                     op0=ALU.subtract, op1=ALU.add,
                 )
 
+            def larger(g):
+                nc.vector.tensor_tensor(
+                    out=value[:, 2 * g : 2 * g + 2, :], in0=value[:, 2 * g : 2 * g + 2, :],
+                    in1=neg_mid[:], op=ALU.max,
+                )
+
             def sides():
-                for h in range(2):
+                for r in range(PAIRS):
                     nc.vector.tensor_scalar(
-                        out=side[:, h, :], in0=xt, scalar1=-2.2 + 0.4 * (2 * g + h + PAIRS),
+                        out=side[:, r, :], in0=xt, scalar1=-2.2 + 0.4 * (r + PAIRS),
                         scalar2=0.5, op0=ALU.is_lt, op1=ALU.subtract,
                     )
 
-            def larger():
-                nc.vector.tensor_tensor(out=value[:], in0=value[:], in1=neg_mid[:], op=ALU.max)
+            def clip():
+                nc.vector.tensor_scalar_min(out=value[:], in0=value[:], scalar1=0.0)
 
             def quantise_silu():
                 nc.vector.quantize_mx(
@@ -200,20 +198,6 @@ def tile_generatorhead_pb_t_kernel(tc, h_norm, base_w2, spline_w2, out):
                     scales=scales[:, SILU_PASS, :],
                     in_=silu[:],
                 )
-
-            def clip():
-                nc.vector.tensor_scalar_min(out=value[:], in0=value[:], scalar1=0.0)
-
-            front = [lambda: outer(0), lambda: outer(1)]
-            if g == 0:
-                front += [middle, middle_even, middle_odd, sides, larger, quantise_silu, clip]
-            else:
-                front += [sides, larger, clip]
-
-            basis = [
-                single.tile([P, 2, cols], BF16, align_bytes=64, name="basis%d" % s)
-                for s in range(2)
-            ]
 
             def signs():
                 nc.vector.tensor_tensor(out=value[:], in0=value[:], in1=side[:], op=ALU.mult)
@@ -225,17 +209,19 @@ def tile_generatorhead_pb_t_kernel(tc, h_norm, base_w2, spline_w2, out):
                 )
 
             def quantise(s):
-                q = s * PAIRS + 2 * g
+                q = s * PAIRS
                 nc.vector.quantize_mx(
-                    out=codes[:, q : q + 2, :].rearrange("p q s -> p (q s)").bitcast(FP8X4),
-                    scales=scales[:, q : q + 2, :].rearrange("p q s -> p (q s)"),
-                    in_=basis[s][:].rearrange("p h f -> p (h f)"),
+                    out=codes[:, q : q + PAIRS, :].rearrange("p q s -> p (q s)").bitcast(FP8X4),
+                    scales=scales[:, q : q + PAIRS, :].rearrange("p q s -> p (q s)"),
+                    in_=basis[s][:].rearrange("p r f -> p (r f)"),
                 )
 
-            back = [
+            before = [lambda: outer(0), middle, middle_odd, middle_even, lambda: larger(0)]
+            after = [lambda: outer(1), quantise_silu, lambda: larger(1), sides, clip]
+            ending = [
                 signs, lambda: split(0), lambda: split(1), lambda: quantise(0), lambda: quantise(1)
             ]
-            return front, back
+            return before, after, ending, codes, scales
 
         def weave(first, second):
             for i in range(max(len(first), len(second))):
@@ -265,23 +251,14 @@ def tile_generatorhead_pb_t_kernel(tc, h_norm, base_w2, spline_w2, out):
                 accs.append(acc)
             return accs
 
-        def store_steps(k, accs):
+        def store(k, accs):
             tiles = CHUNKS[k]
-            result = single.tile([P, tiles, OUTPUTS], F32, name="result")
-
-            def copy_out(b, copy):
-                j, count = banks_of(k)[b]
-                copy(out=result[:, j : j + count, :], in_=accs[b][:])
-
-            def send():
-                nc.sync.dma_start(
-                    out=y[starts[k] : starts[k] + tiles * P, :].rearrange(
-                        "(p j) o -> p j o", j=tiles
-                    ),
-                    in_=result[:],
-                )
-
-            return copy_out, send
+            result = double.tile([P, tiles, OUTPUTS], F32, name="result")
+            nc.vector.tensor_copy(out=result[:], in_=accs[0][:])
+            nc.sync.dma_start(
+                out=y[starts[k] : starts[k] + tiles * P, :].rearrange("(p j) o -> p j o", j=tiles),
+                in_=result[:],
+            )
 
         with tc.manual_schedule():
             raws = {0: load_tokens(0)}
@@ -302,8 +279,7 @@ def tile_generatorhead_pb_t_kernel(tc, h_norm, base_w2, spline_w2, out):
             def regroup_next(k, banks):
                 xts[k] = regroup_tokens(k, banks)
 
-            parts, second_half = scalar_part(0, xts[0])
-            second_half([lambda: regroup_next(1, banks)])
+            parts = scalar_part(0, xts[0], lambda: regroup_next(1, banks))
 
             spline_by_c = double.tile(
                 [P, 2, BASIS, FEATURES], BF16, align_bytes=64, name="codes"
@@ -327,45 +303,29 @@ def tile_generatorhead_pb_t_kernel(tc, h_norm, base_w2, spline_w2, out):
                 )
 
             back = []
-            finished = None
+            finished = {}
             for k in range(len(CHUNKS)):
-                size = CHUNKS[k] * P
-                codes = double.tile([P, PASSES, size], U32, align_bytes=64, name="codes")
-                scales = double.tile([P, PASSES, size], U8, align_bytes=64, name="scales")
-                neg_mid = single.tile([P, 2, size * PACK], BF16, name="neg_mid")
-                state = (codes, scales, neg_mid)
-
-                front, next_back = group_steps(k, 0, xts[k], state, parts)
-                weave(front, back)
-                if k > 0:
-                    finished = multiply(k - 1, *before)
-                back = next_back
                 if k + 2 <= last:
                     banks = turn_tokens(k + 2, load_tokens(k + 2))
                 if k < last:
-                    next_parts, second_half = scalar_part(k + 1, xts[k + 1])
-
-                front, next_back = group_steps(k, 1, xts[k], state, parts)
-                weave(front, back)
-                back = next_back
-                inserts = []
+                    next_parts = scalar_part(
+                        k + 1,
+                        xts[k + 1],
+                        (lambda: regroup_next(k + 2, banks)) if k + 2 <= last else (lambda: None),
+                    )
+                first, rest, ending, codes, scales = vector_steps(k, xts[k], parts)
+                weave(first, back)
+                for step in rest:
+                    step()
                 if k > 0:
-                    copy_out, send = store_steps(k - 1, finished)
-                    for b in range(len(banks_of(k - 1))):
-                        inserts.append(lambda b=b, f=copy_out: f(b, nc.vector.tensor_copy))
-                    inserts.append(send)
-                if k + 2 <= last:
-                    inserts.append(lambda k=k, banks=banks: regroup_next(k + 2, banks))
-                if k < last:
-                    second_half(inserts)
-                    parts = next_parts
-                else:
-                    for insert in inserts:
-                        insert()
+                    finished[k - 1] = multiply(k - 1, *before)
+                if k > 1:
+                    store(k - 2, finished[k - 2])
+                back = ending
                 before = (codes, scales)
+                if k < last:
+                    parts = next_parts
             for step in back:
                 step()
-            copy_out, send = store_steps(last, multiply(last, *before))
-            for b in range(len(banks_of(last))):
-                copy_out(b, nc.scalar.copy)
-            send()
+            store(last - 1, finished[last - 1])
+            store(last, multiply(last, *before))

@@ -104,8 +104,7 @@ def tile_generatorhead_pb_t_kernel(tc, h_norm, base_w2, spline_w2, out):
             dist = [triple.tile([P, 2, cols], F32, name="dist%d" % g) for g in range(2)]
             square = [double.tile([P, 2, cols], F32, name="square%d" % g) for g in range(2)]
             near = double.tile([P, cols], F32, name="near")
-            sq_odd = double.tile([P, cols], F32, name="sq_odd")
-            sq_both = double.tile([P, cols], F32, name="sq_both")
+            square_mid = double.tile([P, cols], F32, name="square_mid")
             silu = double.tile([P, cols], BF16, align_bytes=64, name="silu")
 
             def first_fold(r):
@@ -131,20 +130,20 @@ def tile_generatorhead_pb_t_kernel(tc, h_norm, base_w2, spline_w2, out):
             outer_square(0)
             nc.scalar.activation(out=near[:], in_=near[:], func=ACT.Abs, bias=-1.0)
             second_fold(1)
-            nc.scalar.activation(out=sq_odd[:], in_=near[:], func=ACT.Square)
             nc.scalar.activation(out=silu[:], in_=xt, func=ACT.Silu)
-            nc.scalar.activation(out=sq_both[:], in_=near[:], func=ACT.Square, bias=-0.5)
+            nc.scalar.activation(out=square_mid[:], in_=near[:], func=ACT.Square, bias=-0.5)
             insert()
             outer_square(1)
-            return dist, square, near, sq_odd, sq_both, silu
+            return dist, square, near, square_mid, silu
 
         def vector_steps(k, xt, parts):
-            dist, square, near, sq_odd, sq_both, silu = parts
+            dist, square, near, square_mid, silu = parts
             size = CHUNKS[k] * P
             cols = size * PACK
             codes = double.tile([P, PASSES, size], U32, align_bytes=64, name="codes")
             scales = double.tile([P, PASSES, size], U8, align_bytes=64, name="scales")
             neg_mid = single.tile([P, 2, cols], BF16, name="neg_mid")
+            cubic = single.tile([P, cols], F32, name="cubic")
             value = double.tile([P, PAIRS, cols], BF16, align_bytes=64, name="value")
             side = single.tile([P, PAIRS, cols], BF16, name="side")
             basis = [
@@ -160,20 +159,20 @@ def tile_generatorhead_pb_t_kernel(tc, h_norm, base_w2, spline_w2, out):
 
             def middle():
                 nc.vector.scalar_tensor_tensor(
-                    out=sq_odd[:], in0=near[:], scalar=2.0, in1=sq_odd[:],
+                    out=cubic[:], in0=square_mid[:], scalar=1.25, in1=near[:],
                     op0=ALU.subtract, op1=ALU.mult,
                 )
 
-            def middle_odd():
+            def middle_even():
                 nc.vector.tensor_scalar(
-                    out=neg_mid[:, 1, :], in0=sq_odd[:], scalar1=-1.0, scalar2=-4.0 / 3.0,
-                    op0=ALU.mult, op1=ALU.add,
+                    out=neg_mid[:, 0, :], in0=cubic[:], scalar1=1.0 / 3.0, scalar2=None,
+                    op0=ALU.subtract,
                 )
 
-            def middle_even():
+            def middle_odd():
                 nc.vector.scalar_tensor_tensor(
-                    out=neg_mid[:, 0, :], in0=sq_both[:], scalar=7.0 / 12.0, in1=sq_odd[:],
-                    op0=ALU.subtract, op1=ALU.add,
+                    out=neg_mid[:, 1, :], in0=square_mid[:], scalar=19.0 / 12.0, in1=cubic[:],
+                    op0=ALU.subtract, op1=ALU.subtract,
                 )
 
             def larger(g):
@@ -216,7 +215,7 @@ def tile_generatorhead_pb_t_kernel(tc, h_norm, base_w2, spline_w2, out):
                     in_=basis[s][:].rearrange("p r f -> p (r f)"),
                 )
 
-            before = [lambda: outer(0), middle, middle_odd, middle_even, lambda: larger(0)]
+            before = [lambda: outer(0), middle, middle_even, middle_odd, lambda: larger(0)]
             after = [lambda: outer(1), quantise_silu, lambda: larger(1), sides, clip]
             ending = [
                 signs, lambda: split(0), lambda: split(1), lambda: quantise(0), lambda: quantise(1)
@@ -254,7 +253,7 @@ def tile_generatorhead_pb_t_kernel(tc, h_norm, base_w2, spline_w2, out):
         def store(k, accs):
             tiles = CHUNKS[k]
             result = double.tile([P, tiles, OUTPUTS], F32, name="result")
-            nc.vector.tensor_copy(out=result[:], in_=accs[0][:])
+            nc.scalar.copy(out=result[:], in_=accs[0][:])
             nc.sync.dma_start(
                 out=y[starts[k] : starts[k] + tiles * P, :].rearrange("(p j) o -> p j o", j=tiles),
                 in_=result[:],
@@ -273,12 +272,23 @@ def tile_generatorhead_pb_t_kernel(tc, h_norm, base_w2, spline_w2, out):
             raws[1] = load_tokens(1)
 
             xt = regroup_tokens(0, turn_tokens(0, raws[0]))
-            banks = turn_tokens(1, raws[1])
             xts = {0: xt}
 
             def regroup_next(k, banks):
                 xts[k] = regroup_tokens(k, banks)
 
+            def prepare_pass(q, rows):
+                w_bank = turn_words(w_turned, rows)
+                w_grouped = double.tile([P, OUTPUTS, PACK], BF16, align_bytes=64, name="value")
+                regroup(nc.vector.tensor_copy, w_bank, 2, w_grouped[:])
+                nc.vector.quantize_mx(
+                    out=w_codes[:, q, :].bitcast(FP8X4),
+                    scales=w_scales[:, q, :],
+                    in_=w_grouped[:].rearrange("p o t -> p (o t)"),
+                )
+
+            prepare_pass(SILU_PASS, [base_raw[:, n, :] for n in range(2)])
+            banks = turn_tokens(1, raws[1])
             parts = scalar_part(0, xts[0], lambda: regroup_next(1, banks))
 
             spline_by_c = double.tile(
@@ -289,18 +299,8 @@ def tile_generatorhead_pb_t_kernel(tc, h_norm, base_w2, spline_w2, out):
                     out=spline_by_c[:, n, :, :],
                     in_=spline_raw[:, n, :].rearrange("o (i c) -> o c i", c=BASIS),
                 )
-            for q in [SILU_PASS] + list(range(BASIS)):
-                w_bank = turn_words(
-                    w_turned,
-                    [base_raw[:, n, :] if q == SILU_PASS else spline_by_c[:, n, q, :] for n in range(2)],
-                )
-                w_grouped = double.tile([P, OUTPUTS, PACK], BF16, align_bytes=64, name="value")
-                regroup(nc.vector.tensor_copy, w_bank, 2, w_grouped[:])
-                nc.vector.quantize_mx(
-                    out=w_codes[:, q, :].bitcast(FP8X4),
-                    scales=w_scales[:, q, :],
-                    in_=w_grouped[:].rearrange("p o t -> p (o t)"),
-                )
+            for c in range(BASIS):
+                prepare_pass(c, [spline_by_c[:, n, c, :] for n in range(2)])
 
             back = []
             finished = {}

@@ -130,8 +130,8 @@ def tile_generatorhead_pb_t_kernel(tc, h_norm, base_w2, spline_w2, out):
             outer_square(0)
             nc.scalar.activation(out=near[:], in_=near[:], func=ACT.Abs, bias=-1.0)
             second_fold(1)
-            nc.scalar.activation(out=silu[:], in_=xt, func=ACT.Silu)
             nc.scalar.activation(out=square_mid[:], in_=near[:], func=ACT.Square, bias=-0.5)
+            nc.scalar.activation(out=silu[:], in_=xt, func=ACT.Silu)
             insert()
             outer_square(1)
             return dist, square, near, square_mid, silu
@@ -175,10 +175,11 @@ def tile_generatorhead_pb_t_kernel(tc, h_norm, base_w2, spline_w2, out):
                     op0=ALU.subtract, op1=ALU.subtract,
                 )
 
-            def larger(g):
+            def larger():
+                halves = value[:].rearrange("p (h c) f -> p h c f", h=2)
                 nc.vector.tensor_tensor(
-                    out=value[:, 2 * g : 2 * g + 2, :], in0=value[:, 2 * g : 2 * g + 2, :],
-                    in1=neg_mid[:], op=ALU.max,
+                    out=halves, in0=halves,
+                    in1=neg_mid[:].unsqueeze(1).to_broadcast([P, 2, 2, cols]), op=ALU.max,
                 )
 
             def sides():
@@ -215,8 +216,8 @@ def tile_generatorhead_pb_t_kernel(tc, h_norm, base_w2, spline_w2, out):
                     in_=basis[s][:].rearrange("p r f -> p (r f)"),
                 )
 
-            before = [lambda: outer(0), middle, middle_even, middle_odd, lambda: larger(0)]
-            after = [lambda: outer(1), quantise_silu, lambda: larger(1), sides, clip]
+            before = [lambda: outer(0), middle, middle_even, middle_odd, lambda: outer(1)]
+            after = [quantise_silu, larger, sides, clip]
             ending = [
                 signs, lambda: split(0), lambda: split(1), lambda: quantise(0), lambda: quantise(1)
             ]
@@ -261,14 +262,14 @@ def tile_generatorhead_pb_t_kernel(tc, h_norm, base_w2, spline_w2, out):
 
         with tc.manual_schedule():
             raws = {0: load_tokens(0)}
+            base_raw = const.tile([P, 2, FEATURES], BF16)
+            nc.sync.dma_start(out=base_raw[:], in_=base_w2.rearrange("(n o) i -> o n i", n=2))
             spline_raw = double.tile([P, 2, FEATURES * BASIS], BF16, align_bytes=64, name="codes")
             for n in range(2):
-                nc.scalar.dma_start(
+                nc.sync.dma_start(
                     out=spline_raw[:, n, :],
                     in_=spline_w2[n * P : (n + 1) * P, :, :].rearrange("o i c -> o (i c)"),
                 )
-            base_raw = const.tile([P, 2, FEATURES], BF16)
-            nc.sync.dma_start(out=base_raw[:], in_=base_w2.rearrange("(n o) i -> o n i", n=2))
             raws[1] = load_tokens(1)
 
             xt = regroup_tokens(0, turn_tokens(0, raws[0]))
@@ -277,30 +278,45 @@ def tile_generatorhead_pb_t_kernel(tc, h_norm, base_w2, spline_w2, out):
             def regroup_next(k, banks):
                 xts[k] = regroup_tokens(k, banks)
 
-            def prepare_pass(q, rows):
-                w_bank = turn_words(w_turned, rows)
-                w_grouped = double.tile([P, OUTPUTS, PACK], BF16, align_bytes=64, name="value")
-                regroup(nc.vector.tensor_copy, w_bank, 2, w_grouped[:])
+            def quantise_passes(first, w_grouped):
+                count = w_grouped.shape[1]
+                passes = slice(first, first + count)
                 nc.vector.quantize_mx(
-                    out=w_codes[:, q, :].bitcast(FP8X4),
-                    scales=w_scales[:, q, :],
-                    in_=w_grouped[:].rearrange("p o t -> p (o t)"),
+                    out=w_codes[:, passes, :].rearrange("p q o -> p (q o)").bitcast(FP8X4),
+                    scales=w_scales[:, passes, :].rearrange("p q o -> p (q o)"),
+                    in_=w_grouped.rearrange("p q o t -> p (q o t)"),
                 )
 
-            prepare_pass(SILU_PASS, [base_raw[:, n, :] for n in range(2)])
+            w_base = double.tile([P, 1, OUTPUTS, PACK], BF16, align_bytes=64, name="value")
+            w_bank = turn_words(w_turned, [base_raw[:, n, :] for n in range(2)])
+            regroup(nc.vector.tensor_copy, w_bank, 2, w_base[:, 0, :, :])
+            quantise_passes(SILU_PASS, w_base[:])
             banks = turn_tokens(1, raws[1])
             parts = scalar_part(0, xts[0], lambda: regroup_next(1, banks))
 
-            spline_by_c = double.tile(
-                [P, 2, BASIS, FEATURES], BF16, align_bytes=64, name="codes"
-            )
+            w_grouped = [
+                double.tile([P, PAIRS, OUTPUTS, PACK], BF16, align_bytes=64, name="value")
+                for half in range(2)
+            ]
             for n in range(2):
-                nc.vector.tensor_copy(
-                    out=spline_by_c[:, n, :, :],
-                    in_=spline_raw[:, n, :].rearrange("o (i c) -> o c i", c=BASIS),
-                )
-            for c in range(BASIS):
-                prepare_pass(c, [spline_by_c[:, n, c, :] for n in range(2)])
+                words = spline_raw[:, n, :].bitcast(F32).rearrange("o (i d) -> o d i", d=PAIRS)
+                for d in range(PAIRS):
+                    bank = w_turned.tile([P, PACK, P], F32, name="bank")
+                    for t in range(PACK):
+                        first = (t // 2) * 2 * P + t % 2
+                        nc.tensor.transpose(
+                            bank[:, t, :], words[:, d, first : first + 2 * P - 1 : 2], ident[:]
+                        )
+                    e = 2 * (d % 2)
+                    nc.vector.tensor_copy(
+                        out=w_grouped[d // 2][:, e : e + 2, n * P : (n + 1) * P, :],
+                        in_=bank[:]
+                        .rearrange("p t o -> p (t o)")
+                        .bitcast(BF16)
+                        .rearrange("p (t o h) -> p h o t", t=PACK, h=2),
+                    )
+            for half in range(2):
+                quantise_passes(half * PAIRS, w_grouped[half][:])
 
             back = []
             finished = {}

@@ -25,6 +25,11 @@ HALVES = 2
 CHUNKS = [1] + [2] * 15 + [1]
 BANK_TILES = 2
 
+ORDER = [
+    "side0", "side1", "signs", "side2", "side3", "split0", "outer0", "codes0", "middle", "split1",
+    "even", "odd", "outer1", "silu", "larger", "codes1", "clip",
+]
+
 FLOPS = 2 * TOKENS * OUTPUTS * FEATURES * PASSES
 
 
@@ -145,7 +150,7 @@ def tile_generatorhead_pb_t_kernel(tc, h_norm, base_w2, spline_w2, out):
             neg_mid = single.tile([P, 2, cols], BF16, name="neg_mid")
             cubic = single.tile([P, cols], F32, name="cubic")
             value = double.tile([P, PAIRS, cols], BF16, align_bytes=64, name="value")
-            side = single.tile([P, PAIRS, cols], BF16, name="side")
+            side = double.tile([P, PAIRS, cols], BF16, name="side")
             basis = [
                 single.tile([P, PAIRS, cols], BF16, align_bytes=64, name="basis%d" % s)
                 for s in range(2)
@@ -182,12 +187,11 @@ def tile_generatorhead_pb_t_kernel(tc, h_norm, base_w2, spline_w2, out):
                     in1=neg_mid[:].unsqueeze(1).to_broadcast([P, 2, 2, cols]), op=ALU.max,
                 )
 
-            def sides():
-                for r in range(PAIRS):
-                    nc.vector.tensor_scalar(
-                        out=side[:, r, :], in0=xt, scalar1=-2.2 + 0.4 * (r + PAIRS),
-                        scalar2=0.5, op0=ALU.is_lt, op1=ALU.subtract,
-                    )
+            def make_side(r):
+                nc.vector.tensor_scalar(
+                    out=side[:, r, :], in0=xt, scalar1=-2.2 + 0.4 * (r + PAIRS),
+                    scalar2=0.5, op0=ALU.is_lt, op1=ALU.subtract,
+                )
 
             def clip():
                 nc.vector.tensor_scalar_min(out=value[:], in0=value[:], scalar1=0.0)
@@ -216,19 +220,18 @@ def tile_generatorhead_pb_t_kernel(tc, h_norm, base_w2, spline_w2, out):
                     in_=basis[s][:].rearrange("p r f -> p (r f)"),
                 )
 
-            before = [lambda: outer(0), middle, middle_even, middle_odd, lambda: outer(1)]
-            after = [quantise_silu, larger, sides, clip]
-            ending = [
-                signs, lambda: split(0), lambda: split(1), lambda: quantise(0), lambda: quantise(1)
-            ]
-            return before, after, ending, codes, scales
-
-        def weave(first, second):
-            for i in range(max(len(first), len(second))):
-                if i < len(first):
-                    first[i]()
-                if i < len(second):
-                    second[i]()
+            steps = {
+                "outer0": lambda: outer(0), "outer1": lambda: outer(1), "middle": middle,
+                "even": middle_even, "odd": middle_odd, "larger": larger, "clip": clip,
+                "silu": quantise_silu, "side0": lambda: make_side(0),
+                "side1": lambda: make_side(1), "side2": lambda: make_side(2),
+                "side3": lambda: make_side(3),
+            }
+            ending = {
+                "signs": signs, "split0": lambda: split(0), "split1": lambda: split(1),
+                "codes0": lambda: quantise(0), "codes1": lambda: quantise(1),
+            }
+            return steps, ending, codes, scales
 
         def multiply(k, codes, scales):
             accs = []
@@ -270,7 +273,8 @@ def tile_generatorhead_pb_t_kernel(tc, h_norm, base_w2, spline_w2, out):
                     out=spline_raw[:, n, :],
                     in_=spline_w2[n * P : (n + 1) * P, :, :].rearrange("o i c -> o (i c)"),
                 )
-            raws[1] = load_tokens(1)
+                if n == 0:
+                    raws[1] = load_tokens(1)
 
             xt = regroup_tokens(0, turn_tokens(0, raws[0]))
             xts = {0: xt}
@@ -291,14 +295,13 @@ def tile_generatorhead_pb_t_kernel(tc, h_norm, base_w2, spline_w2, out):
             w_bank = turn_words(w_turned, [base_raw[:, n, :] for n in range(2)])
             regroup(nc.vector.tensor_copy, w_bank, 2, w_base[:, 0, :, :])
             quantise_passes(SILU_PASS, w_base[:])
-            banks = turn_tokens(1, raws[1])
-            parts = scalar_part(0, xts[0], lambda: regroup_next(1, banks))
-
             w_grouped = [
                 double.tile([P, PAIRS, OUTPUTS, PACK], BF16, align_bytes=64, name="value")
                 for half in range(2)
             ]
             for n in range(2):
+                if n == 1:
+                    banks = turn_tokens(1, raws[1])
                 words = spline_raw[:, n, :].bitcast(F32).rearrange("o (i d) -> o d i", d=PAIRS)
                 for d in range(PAIRS):
                     bank = w_turned.tile([P, PACK, P], F32, name="bank")
@@ -318,7 +321,9 @@ def tile_generatorhead_pb_t_kernel(tc, h_norm, base_w2, spline_w2, out):
             for half in range(2):
                 quantise_passes(half * PAIRS, w_grouped[half][:])
 
-            back = []
+            parts = scalar_part(0, xts[0], lambda: regroup_next(1, banks))
+
+            back = {}
             finished = {}
             for k in range(len(CHUNKS)):
                 if k + 2 <= last:
@@ -329,10 +334,12 @@ def tile_generatorhead_pb_t_kernel(tc, h_norm, base_w2, spline_w2, out):
                         xts[k + 1],
                         (lambda: regroup_next(k + 2, banks)) if k + 2 <= last else (lambda: None),
                     )
-                first, rest, ending, codes, scales = vector_steps(k, xts[k], parts)
-                weave(first, back)
-                for step in rest:
-                    step()
+                steps, ending, codes, scales = vector_steps(k, xts[k], parts)
+                for name in ORDER:
+                    if name in steps:
+                        steps[name]()
+                    elif name in back:
+                        back[name]()
                 if k > 0:
                     finished[k - 1] = multiply(k - 1, *before)
                 if k > 1:
@@ -341,7 +348,8 @@ def tile_generatorhead_pb_t_kernel(tc, h_norm, base_w2, spline_w2, out):
                 before = (codes, scales)
                 if k < last:
                     parts = next_parts
-            for step in back:
-                step()
+            for name in ORDER:
+                if name in back:
+                    back[name]()
             store(last - 1, finished[last - 1])
             store(last, multiply(last, *before))

import math
from contextlib import ExitStack

import concourse.mybir as mybir
from concourse.masks import make_identity

F32 = mybir.dt.float32
BF16 = mybir.dt.bfloat16
U32 = mybir.dt.uint32
U8 = mybir.dt.uint8
FP8X4 = mybir.dt.float8_e4m3fn_x4
ACT = mybir.ActivationFunctionType
ALU = mybir.AluOpType

P = 128
PACK = 4
TOKENS = 8 * 512
FEATURES = 512
OUTPUTS = 256
BASIS = 8
PAIRS = BASIS // 2
PASSES = BASIS + 1
SILU_PASS = BASIS
HALVES = 2
CHUNKS = [1] + [2] * 15 + [1]
BANK_TILES = 2

ORDER = [
    "side0", "side1", "signs", "side2", "side3", "split0", "outer0", "codes0", "middle", "split1",
    "even", "odd", "outer1", "silu", "larger", "codes1", "clip",
]

FLOPS = 2 * TOKENS * OUTPUTS * FEATURES * PASSES


def tile_generatorhead_pb_t_kernel(tc, h_norm, base_w2, spline_w2, out):
    nc = tc.nc
    x = h_norm.flatten_outer_dims()
    y = out.flatten_outer_dims()

    with ExitStack() as pools:
        const = pools.enter_context(tc.tile_pool(name="const", bufs=1))
        single = pools.enter_context(tc.tile_pool(name="single", bufs=1))
        double = pools.enter_context(tc.tile_pool(name="double", bufs=2))
        triple = pools.enter_context(tc.tile_pool(name="triple", bufs=3))
        turned = pools.enter_context(tc.psum_pool(name="turned", bufs=2))
        w_turned = pools.enter_context(tc.psum_pool(name="w_turned", bufs=2))
        sums = pools.enter_context(tc.psum_pool(name="sums", bufs=4))

        ident = const.tile([P, P], F32)
        make_identity(nc, ident[:])

        k_outer = 1.0 / math.sqrt(3.0)
        ones = const.tile([P, 1], F32)
        nc.vector.memset(ones[:], 1.0)
        outer_bias = const.tile([P, 1], F32)
        nc.vector.tensor_scalar(
            out=outer_bias[:], in0=ones[:], scalar1=-2.0 * k_outer, scalar2=None, op0=ALU.mult
        )

        def turn_words(pool, rows):
            bank = pool.tile([P, 2, HALVES, P], F32, name="bank")
            for n in range(len(rows)):
                words = rows[n].bitcast(F32)
                for u in range(HALVES):
                    nc.tensor.transpose(bank[:, n, u, :], words[:, u * P : (u + 1) * P], ident[:])
            return bank

        def regroup(copy, bank, count, grouped):
            copy(
                out=grouped.bitcast(F32).rearrange("p (n r) u -> p n r u", n=count),
                in_=bank[:, 0:count, :, :].rearrange("p n u r -> p n r u"),
            )

        starts = [sum(CHUNKS[:k]) * P for k in range(len(CHUNKS))]
        last = len(CHUNKS) - 1

        def banks_of(k):
            return [
                (j, min(BANK_TILES, CHUNKS[k] - j)) for j in range(0, CHUNKS[k], BANK_TILES)
            ]

        def load_tokens(k):
            tiles = CHUNKS[k]
            x_raw = double.tile([P, tiles, FEATURES], BF16, name="x_raw")
            nc.sync.dma_start(
                out=x_raw[:],
                in_=x[starts[k] : starts[k] + tiles * P, :].rearrange("(p j) i -> p j i", j=tiles),
            )
            return x_raw

        def turn_tokens(k, x_raw):
            return [
                turn_words(turned, [x_raw[:, j + n, :] for n in range(count)])
                for j, count in banks_of(k)
            ]

        def regroup_tokens(k, banks):
            x_grouped = triple.tile([P, CHUNKS[k] * P, PACK], BF16, name="x_grouped")
            for bank, (j, count) in zip(banks, banks_of(k)):
                regroup(nc.scalar.copy, bank, count, x_grouped[:, j * P : (j + count) * P, :])
            return x_grouped[:].rearrange("p s t -> p (s t)")

        w_codes = single.tile([P, PASSES, OUTPUTS], U32, align_bytes=64)
        w_scales = single.tile([P, PASSES, OUTPUTS], U8, align_bytes=64)

        def scalar_part(k, xt, insert):
            cols = CHUNKS[k] * P * PACK
            dist = [triple.tile([P, 2, cols], F32, name="dist%d" % g) for g in range(2)]
            square = [double.tile([P, 2, cols], F32, name="square%d" % g) for g in range(2)]
            near = double.tile([P, cols], F32, name="near")
            square_mid = double.tile([P, cols], F32, name="square_mid")
            silu = double.tile([P, cols], BF16, align_bytes=64, name="silu")

            def first_fold(r):
                nc.scalar.activation(
                    out=dist[r // 2][:, r % 2, :], in_=xt, func=ACT.Abs, scale=2.5, bias=1.5 - r
                )

            def second_fold(g):
                nc.scalar.activation(out=dist[g][:], in_=dist[g][:], func=ACT.Abs, bias=-2.0)

            def outer_square(g):
                nc.scalar.activation(
                    out=square[g][:], in_=dist[g][:], func=ACT.Square, scale=k_outer,
                    bias=outer_bias[:],
                )

            first_fold(1)
            first_fold(0)
            first_fold(2)
            second_fold(0)
            first_fold(3)
            nc.scalar.activation(out=near[:], in_=dist[0][:, 1, :], func=ACT.Abs, bias=-1.0)
            outer_square(0)
            nc.scalar.activation(out=near[:], in_=near[:], func=ACT.Abs, bias=-1.0)
            second_fold(1)
            nc.scalar.activation(out=square_mid[:], in_=near[:], func=ACT.Square, bias=-0.5)
            nc.scalar.activation(out=silu[:], in_=xt, func=ACT.Silu)
            insert()
            outer_square(1)
            return dist, square, near, square_mid, silu

        def vector_steps(k, xt, parts):
            dist, square, near, square_mid, silu = parts
            size = CHUNKS[k] * P
            cols = size * PACK
            codes = double.tile([P, PASSES, size], U32, align_bytes=64, name="codes")
            scales = double.tile([P, PASSES, size], U8, align_bytes=64, name="scales")
            neg_mid = single.tile([P, 2, cols], BF16, name="neg_mid")
            cubic = single.tile([P, cols], F32, name="cubic")
            value = double.tile([P, PAIRS, cols], BF16, align_bytes=64, name="value")
            side = double.tile([P, PAIRS, cols], BF16, name="side")
            basis = [
                single.tile([P, PAIRS, cols], BF16, align_bytes=64, name="basis%d" % s)
                for s in range(2)
            ]

            def outer(g):
                nc.vector.scalar_tensor_tensor(
                    out=value[:, 2 * g : 2 * g + 2, :], in0=dist[g][:], scalar=2.0,
                    in1=square[g][:], op0=ALU.subtract, op1=ALU.mult,
                )

            def middle():
                nc.vector.scalar_tensor_tensor(
                    out=cubic[:], in0=square_mid[:], scalar=1.25, in1=near[:],
                    op0=ALU.subtract, op1=ALU.mult,
                )

            def middle_even():
                nc.vector.tensor_scalar(
                    out=neg_mid[:, 0, :], in0=cubic[:], scalar1=1.0 / 3.0, scalar2=None,
                    op0=ALU.subtract,
                )

            def middle_odd():
                nc.vector.scalar_tensor_tensor(
                    out=neg_mid[:, 1, :], in0=square_mid[:], scalar=19.0 / 12.0, in1=cubic[:],
                    op0=ALU.subtract, op1=ALU.subtract,
                )

            def larger():
                halves = value[:].rearrange("p (h c) f -> p h c f", h=2)
                nc.vector.tensor_tensor(
                    out=halves, in0=halves,
                    in1=neg_mid[:].unsqueeze(1).to_broadcast([P, 2, 2, cols]), op=ALU.max,
                )

            def make_side(r):
                nc.vector.tensor_scalar(
                    out=side[:, r, :], in0=xt, scalar1=-2.2 + 0.4 * (r + PAIRS),
                    scalar2=0.5, op0=ALU.is_lt, op1=ALU.subtract,
                )

            def clip():
                nc.vector.tensor_scalar_min(out=value[:], in0=value[:], scalar1=0.0)

            def quantise_silu():
                nc.vector.quantize_mx(
                    out=codes[:, SILU_PASS, :].bitcast(FP8X4),
                    scales=scales[:, SILU_PASS, :],
                    in_=silu[:],
                )

            def signs():
                nc.vector.tensor_tensor(out=value[:], in0=value[:], in1=side[:], op=ALU.mult)

            def split(s):
                nc.vector.tensor_scalar(
                    out=basis[s][:], in0=value[:], scalar1=-1.0 if s == 0 else 1.0, scalar2=0.0,
                    op0=ALU.mult, op1=ALU.max,
                )

            def quantise(s):
                q = s * PAIRS
                nc.vector.quantize_mx(
                    out=codes[:, q : q + PAIRS, :].rearrange("p q s -> p (q s)").bitcast(FP8X4),
                    scales=scales[:, q : q + PAIRS, :].rearrange("p q s -> p (q s)"),
                    in_=basis[s][:].rearrange("p r f -> p (r f)"),
                )

            steps = {
                "outer0": lambda: outer(0), "outer1": lambda: outer(1), "middle": middle,
                "even": middle_even, "odd": middle_odd, "larger": larger, "clip": clip,
                "silu": quantise_silu, "side0": lambda: make_side(0),
                "side1": lambda: make_side(1), "side2": lambda: make_side(2),
                "side3": lambda: make_side(3),
            }
            ending = {
                "signs": signs, "split0": lambda: split(0), "split1": lambda: split(1),
                "codes0": lambda: quantise(0), "codes1": lambda: quantise(1),
            }
            return steps, ending, codes, scales

        def multiply(k, codes, scales):
            accs = []
            order = [SILU_PASS] + list(range(BASIS))
            for start_tile, count in banks_of(k):
                acc = sums.tile([P, count, OUTPUTS], F32, name="acc")
                for n in range(count):
                    j = start_tile + n
                    slots = slice(j * P, (j + 1) * P)
                    for q in order:
                        nc.tensor.matmul_mx(
                            out=acc[:, n, :],
                            lhsT=codes[:, q, slots].bitcast(FP8X4),
                            lhsT_scale=scales[:, q, slots],
                            rhs=w_codes[:, q, :].bitcast(FP8X4),
                            rhs_scale=w_scales[:, q, :],
                            start=(q == order[0]),
                            stop=(q == order[-1]),
                        )
                accs.append(acc)
            return accs

        def store(k, accs):
            tiles = CHUNKS[k]
            result = double.tile([P, tiles, OUTPUTS], F32, name="result")
            nc.scalar.copy(out=result[:], in_=accs[0][:])
            nc.sync.dma_start(
                out=y[starts[k] : starts[k] + tiles * P, :].rearrange("(p j) o -> p j o", j=tiles),
                in_=result[:],
            )

        with tc.manual_schedule():
            raws = {0: load_tokens(0)}
            base_raw = const.tile([P, 2, FEATURES], BF16)
            nc.sync.dma_start(out=base_raw[:], in_=base_w2.rearrange("(n o) i -> o n i", n=2))
            spline_raw = double.tile([P, 2, FEATURES * BASIS], BF16, align_bytes=64, name="codes")
            for n in range(2):
                nc.sync.dma_start(
                    out=spline_raw[:, n, :],
                    in_=spline_w2[n * P : (n + 1) * P, :, :].rearrange("o i c -> o (i c)"),
                )
                if n == 0:
                    raws[1] = load_tokens(1)

            xt = regroup_tokens(0, turn_tokens(0, raws[0]))
            xts = {0: xt}

            def regroup_next(k, banks):
                xts[k] = regroup_tokens(k, banks)

            def quantise_passes(first, w_grouped):
                count = w_grouped.shape[1]
                passes = slice(first, first + count)
                nc.vector.quantize_mx(
                    out=w_codes[:, passes, :].rearrange("p q o -> p (q o)").bitcast(FP8X4),
                    scales=w_scales[:, passes, :].rearrange("p q o -> p (q o)"),
                    in_=w_grouped.rearrange("p q o t -> p (q o t)"),
                )

            w_base = double.tile([P, 1, OUTPUTS, PACK], BF16, align_bytes=64, name="value")
            w_bank = turn_words(w_turned, [base_raw[:, n, :] for n in range(2)])
            regroup(nc.vector.tensor_copy, w_bank, 2, w_base[:, 0, :, :])
            quantise_passes(SILU_PASS, w_base[:])
            w_grouped = [
                double.tile([P, PAIRS, OUTPUTS, PACK], BF16, align_bytes=64, name="value")
                for half in range(2)
            ]
            for n in range(2):
                if n == 1:
                    banks = turn_tokens(1, raws[1])
                words = spline_raw[:, n, :].bitcast(F32).rearrange("o (i d) -> o d i", d=PAIRS)
                for d in range(PAIRS):
                    bank = w_turned.tile([P, PACK, P], F32, name="bank")
                    for t in range(PACK):
                        first = (t // 2) * 2 * P + t % 2
                        nc.tensor.transpose(
                            bank[:, t, :], words[:, d, first : first + 2 * P - 1 : 2], ident[:]
                        )
                    e = 2 * (d % 2)
                    nc.vector.tensor_copy(
                        out=w_grouped[d // 2][:, e : e + 2, n * P : (n + 1) * P, :],
                        in_=bank[:]
                        .rearrange("p t o -> p (t o)")
                        .bitcast(BF16)
                        .rearrange("p (t o h) -> p h o t", t=PACK, h=2),
                    )
            for half in range(2):
                quantise_passes(half * PAIRS, w_grouped[half][:])

            parts = scalar_part(0, xts[0], lambda: regroup_next(1, banks))

            back = {}
            finished = {}
            for k in range(len(CHUNKS)):
                if k + 2 <= last:
                    banks = turn_tokens(k + 2, load_tokens(k + 2))
                if k < last:
                    next_parts = scalar_part(
                        k + 1,
                        xts[k + 1],
                        (lambda: regroup_next(k + 2, banks)) if k + 2 <= last else (lambda: None),
                    )
                steps, ending, codes, scales = vector_steps(k, xts[k], parts)
                for name in ORDER:
                    if name in steps:
                        steps[name]()
                    elif name in back:
                        back[name]()
                if k > 0:
                    finished[k - 1] = multiply(k - 1, *before)
                if k > 1:
                    store(k - 2, finished[k - 2])
                back = ending
                before = (codes, scales)
                if k < last:
                    parts = next_parts
            for name in ORDER:
                if name in back:
                    back[name]()
            store(last - 1, finished[last - 1])
            store(last, multiply(last, *before))
